import numpy as np
import ml_dtypes


def mxq(x, axis, fmt="e4m3"):
    dtype, down = {"e4m3": (ml_dtypes.float8_e4m3fn, 7), "e5m2": (ml_dtypes.float8_e5m2, 14)}[fmt]
    v = np.moveaxis(np.asarray(x, np.float32).astype(ml_dtypes.bfloat16).astype(np.float64), axis, -1)
    blocks = v.reshape(v.shape[:-1] + (-1, 32))
    amax = np.abs(blocks).max(-1, keepdims=True)
    byte = np.maximum(np.where(amax > 0, np.frexp(amax)[1] - 1 + 127, 0) - down, 1)
    scale = np.exp2(byte - 127.0)
    codes = (blocks / scale).astype(np.float32).astype(dtype).astype(np.float64)
    return np.moveaxis((codes * scale).reshape(v.shape), -1, axis)


WIDE = False


def mx_kscale(k):
    if not WIDE:
        return np.ones(k)
    levels = np.array([10, -10, 5, -5, 0])
    if k % 512:
        return np.exp2(np.random.permutation(np.resize(levels, k // 32))).repeat(32)
    a = np.empty((k // 512, 16))
    for p in range(k // 512):
        a[p, :8] = np.random.permutation(np.resize(levels, 8))
        for g in range(8):
            far = levels[np.abs(levels - a[p, g]) >= 10]
            a[p, g + 8] = far[np.random.randint(len(far))]
    return np.exp2(a.ravel()).repeat(32)


BF16 = ml_dtypes.bfloat16


def bf(x):
    return np.asarray(x, np.float32).astype(BF16)


def f64(x):
    return np.asarray(x).astype(np.float64)


B, C, H, W, P, DIM = 16, 8, 256, 256, 16, 512
SHIFT = P // 2
WD = 5 * C * P * P // 4
N = (H // P) * (W // P)
EPS = 1e-5
XS = 0.015


def patch_shift(x, shift):
    xp = np.pad(x, ((0, 0), (0, 0), (shift, shift), (shift, shift)))
    s2 = 2 * shift
    return np.concatenate([x, xp[:, :, :-s2, :-s2], xp[:, :, :-s2, s2:], xp[:, :, s2:, :-s2], xp[:, :, s2:, s2:]], axis=1)


def haar_detail_mean(x):
    b_, c_, h, w = x.shape
    r = x.reshape(b_, c_, h // 2, 2, w // 2, 2)
    return (3.0 * r[:, :, :, 0, :, 0] - r[:, :, :, 0, :, 1] - r[:, :, :, 1, :, 0] - r[:, :, :, 1, :, 1]) / 6.0


def patchify(x, p):
    b_, c_, hh, ww = x.shape
    h, w = hh // p, ww // p
    return x.reshape(b_, c_, h, p, w, p).transpose(0, 2, 4, 3, 5, 1).reshape(b_, h * w, p * p * c_)


def layernorm(u, g, b):
    m = u.mean(-1, keepdims=True)
    v = np.square(u - m).mean(-1, keepdims=True)
    return (u - m) / np.sqrt(v + EPS) * g + b


def setup_inputs():
    s = mx_kscale(WD)
    return {"x": bf(np.random.standard_normal((B, C, H, W)) * XS),
            "ln2_g": bf((1.0 + 0.1 * np.random.standard_normal(WD)) * s),
            "ln2_b": bf(0.1 * np.random.standard_normal(WD) * s),
            "w2": bf(np.random.standard_normal((WD, DIM)) / np.sqrt(WD) / s[:, None]),
            "b2": bf(0.3 * np.random.standard_normal(DIM)),
            "tok": bf(np.random.standard_normal((B, N, DIM)))}


def reference(x, ln2_g, ln2_b, w2, b2, tok):
    waves = haar_detail_mean(patch_shift(f64(x), SHIFT))
    z = layernorm(patchify(waves, P // 2), f64(ln2_g), f64(ln2_b))
    wtok = (mxq(z, 2, "e4m3") @ mxq(f64(w2), 0, "e4m3")) + f64(b2)
    return f64(tok) + wtok

@@ -1,0 +1,372 @@
+from contextlib import ExitStack
+
+import concourse.mybir as mybir
+from concourse.masks import make_identity
+
+F32 = mybir.dt.float32
+BF16 = mybir.dt.bfloat16
+U32 = mybir.dt.uint32
+U8 = mybir.dt.uint8
+FP8X4 = mybir.dt.float8_e4m3fn_x4
+ALU = mybir.AluOpType
+ACT = mybir.ActivationFunctionType
+AX = mybir.AxisListType
+
+P = 128
+KDIM = 2560
+DIM = 512
+FLOPS = 2 * 4096 * KDIM * DIM
+
+ROW0 = (4, 0, 0, 8, 8)
+COL0 = (4, 0, 8, 0, 8)
+S_SLOTS = (1, 5, 9)
+ORDER = (6, 7, 0, 1, 2, 3, 4, 5)
+
+
+def tile_shiftedpatchtokenization_pb_t_kernel(tc, x, ln2_g, ln2_b, w2, b2, tok, out):
+    nc = tc.nc
+    xv = x.rearrange("b c (g u r) w -> (b c) g u (r w)", g=8, u=8)
+    wv = w2.rearrange("(y g t q) n -> g q y t n", y=16, g=5, t=4)
+    tok_v = tok.rearrange("b (g e j) d -> (b g) e j d", g=8, e=2)
+    out_v = out.rearrange("b (g e j) d -> (b g) e j d", g=8, e=2)
+
+    with ExitStack() as ctx:
+        keep = ctx.enter_context(tc.tile_pool(name="keep", bufs=1))
+        ident = keep.tile([P, P], F32)
+        sh_dn = keep.tile([P, P], F32)
+        sh_up = keep.tile([P, P], F32)
+        gb = keep.tile([P, P], F32)
+        b2bc = keep.tile([P, DIM], BF16)
+        wc = keep.tile([P, 5, DIM], U32, align_bytes=64)
+        ws = keep.tile([P, 5, DIM], U8, align_bytes=64)
+        W = keep.tile([P, 24, 136, 8], F32)
+        CS = keep.tile([P, 2, 4, 32], F32)
+        CR = keep.tile([P, 2, 6, 34], F32)
+        A1 = keep.tile([P, 2, 5, 34], F32)
+        Rw = keep.tile([P, 2, 2, 34], F32)
+        Bw = keep.tile([P, 2, 2, 33], F32)
+        Bc = keep.tile([P, 2, 2, 33], F32)
+        ST = keep.tile([P, 2, 2, 16], F32)
+        mean = keep.tile([P, 32], F32)
+        va = keep.tile([P, 32], F32)
+        tmp = keep.tile([P, 32], F32)
+        rstd = keep.tile([P, 32], F32)
+        nbias = keep.tile([P, 32], F32)
+        one = keep.tile([P, 1], F32)
+        mask_top = keep.tile([P, 1], F32)
+        mask_bot = keep.tile([P, 1], F32)
+        neg_id = keep.tile([P, P], BF16)
+
+        nc.vector.memset(one[:], 1.0)
+        nc.scalar.sqrt(one[:], one[:])
+
+        make_identity(nc, ident[:])
+        id8 = ident[:].rearrange("p (a b) -> p a b", b=8)
+        nc.vector.tensor_scalar(out=neg_id[:], in0=ident[:], scalar1=-1.0, scalar2=None, op0=ALU.mult)
+        nc.vector.memset(sh_dn[:], 0.0)
+        nc.vector.memset(sh_up[:], 0.0)
+        nc.vector.tensor_copy(out=sh_dn[:, 1:P], in_=ident[:, 0 : P - 1])
+        nc.vector.tensor_copy(out=sh_up[:, 0 : P - 1], in_=ident[:, 1:P])
+        nc.vector.memset(sh_dn[:].rearrange("p (a b) -> p a b", b=8)[:, :, 0:1], 0.0)
+        nc.vector.memset(sh_up[:].rearrange("p (a b) -> p a b", b=8)[:, :, 7:8], 0.0)
+        nc.vector.tensor_reduce(out=mask_top[:], in_=id8[:, :, 0], axis=AX.X, op=ALU.add)
+        nc.vector.tensor_reduce(out=mask_bot[:], in_=id8[:, :, 7], axis=AX.X, op=ALU.add)
+        nc.vector.tensor_scalar(out=mask_top[:], in0=mask_top[:], scalar1=-1.0, scalar2=1.0, op0=ALU.mult, op1=ALU.add)
+        nc.vector.tensor_scalar(out=mask_bot[:], in0=mask_bot[:], scalar1=-1.0, scalar2=1.0, op0=ALU.mult, op1=ALU.add)
+        nc.vector.memset(W[:, :, 0:4, :], 0.0)
+        nc.vector.memset(W[:, :, 132:136, :], 0.0)
+        nc.vector.memset(CR[:], 0.0)
+        nc.vector.memset(CS[:], 0.0)
+
+        with ExitStack() as pa:
+            xpool = pa.enter_context(tc.tile_pool(name="xpool", bufs=3))
+            hpool = pa.enter_context(tc.tile_pool(name="hpool", bufs=2))
+            tpool = pa.enter_context(tc.tile_pool(name="tpool", bufs=1))
+            psa = pa.enter_context(tc.psum_pool(name="psa", bufs=3))
+            psx = pa.enter_context(tc.psum_pool(name="psx", bufs=2))
+
+            m_a = tpool.tile([P, 2056], F32)
+            m_b = tpool.tile([P, 2056], F32)
+            for m_t in (m_a, m_b):
+                nc.vector.memset(m_t[:, 0:4], 0.0)
+                nc.vector.memset(m_t[:, 2052:2056], 0.0)
+            g0b = tpool.tile([P, P], BF16)
+            g0f = tpool.tile([P, P], F32)
+            nc.vector.memset(g0b[:], 0.0)
+            bns = tpool.tile([P, 4, 32, 6], F32)
+            sq_a = tpool.tile([P, 32], F32)
+            sq_b = tpool.tile([P, 32], F32)
+            wpool = pa.enter_context(tc.tile_pool(name="wpool", bufs=2))
+            wraws = {}
+            wgrps = {}
+
+            pa.enter_context(tc.manual_schedule())
+            xss = {}
+            hs = {}
+
+            def load_chunk(i):
+                xs = xpool.tile([P, 8, 1024], BF16, name="xs")
+                nc.sync.dma_start(out=xs[:], in_=xv[:, :, ORDER[i], :])
+                xss[i] = xs
+
+            def haar(i):
+                xq = xss[i][:].rearrange("p g (o e x f) -> p g o e x f", o=2, e=2, x=128, f=2)
+                h = hpool.tile([P, 8, 2, 128], F32, name="h")
+                nc.vector.scalar_tensor_tensor(
+                    out=h[:], in0=xq[:, :, :, 0, :, 0], scalar=3.0, in1=xq[:, :, :, 0, :, 1],
+                    op0=ALU.mult, op1=ALU.subtract,
+                )
+                nc.vector.tensor_tensor(out=h[:], in0=h[:], in1=xq[:, :, :, 1, :, 0], op=ALU.subtract)
+                hs[i] = h
+
+            def turn_first(i):
+                h = hs[i]
+                xq = xss[i][:].rearrange("p g (o e x f) -> p g o e x f", o=2, e=2, x=128, f=2)
+                m_t = m_a if i % 2 == 0 else m_b
+                m_v = m_t[:, 4:2052].rearrange("p (c o b g) -> p c o b g", c=8, o=2, b=16)
+                for o in range(2):
+                    for hq in range(2):
+                        p1 = psa.tile([P, 4, P], F32, name="p1")
+                        for gq in range(4):
+                            nc.tensor.matmul(
+                                out=p1[:, gq, :], lhsT=h[:, 4 * hq + gq, o, :], rhs=ident[:],
+                                is_transpose=True, start=(gq == 0), stop=False,
+                            )
+                        for gq in range(4):
+                            nc.tensor.matmul(
+                                out=p1[:, gq, :], lhsT=xq[:, 4 * hq + gq, o, 1, :, 1], rhs=neg_id[:],
+                                start=False, stop=(gq == 3),
+                            )
+                        nc.scalar.copy(
+                            out=m_v[:, :, o, :, 4 * hq : 4 * hq + 4],
+                            in_=p1[:].rearrange("p q (b c) -> p c b q", c=8),
+                        )
+
+            def turn_second(i):
+                u = ORDER[i]
+                m_t = m_a if i % 2 == 0 else m_b
+                for o in range(2):
+                    ro = 2 * u + o
+                    jobs = [(4 + ro, 0, None)]
+                    if ro < 4:
+                        jobs.append((20 + ro, 1, mask_bot))
+                    if ro >= 12:
+                        jobs.append((ro - 12, -1, mask_top))
+                    for r, shift, mask in jobs:
+                        for ch in range(2):
+                            p2 = psa.tile([P, 4, P], F32, name="p2")
+                            for c4 in range(4):
+                                base = 4 + ((4 * ch + c4) * 2 + o) * P + shift
+                                nc.tensor.transpose(p2[:, c4, :], m_t[:, base : base + P], ident[:])
+                            dst = W[:, r, 4:132, 4 * ch : 4 * ch + 4]
+                            srcv = p2[:].rearrange("p c x -> p x c")
+                            if mask is None:
+                                nc.scalar.copy(out=dst, in_=srcv)
+                            else:
+                                nc.scalar.activation(out=dst, in_=srcv, func=ACT.Copy, scale=mask[:, 0:1])
+
+            def cell_sums(q):
+                r0 = 4 + 4 * q
+                for cx in range(32):
+                    nc.vector.bn_stats(out=bns[:, q, cx, :], in_=W[:, r0 : r0 + 4, 4 + 4 * cx : 8 + 4 * cx, :])
+                nc.vector.tensor_tensor(out=CS[:, 0, q, :], in0=bns[:, q, :, 1], in1=bns[:, q, :, 4], op=ALU.add)
+                nc.vector.tensor_tensor(out=sq_a[:], in0=bns[:, q, :, 1], in1=bns[:, q, :, 1], op=ALU.mult)
+                nc.vector.tensor_tensor(out=sq_b[:], in0=bns[:, q, :, 4], in1=bns[:, q, :, 4], op=ALU.mult)
+                nc.vector.tensor_tensor(out=sq_a[:], in0=sq_a[:], in1=sq_b[:], op=ALU.add)
+                nc.vector.tensor_tensor(out=sq_b[:], in0=bns[:, q, :, 2], in1=bns[:, q, :, 5], op=ALU.add)
+                nc.vector.scalar_tensor_tensor(
+                    out=CS[:, 1, q, :], in0=sq_a[:], scalar=64.0, in1=sq_b[:], op0=ALU.mult, op1=ALU.add
+                )
+                nc.vector.tensor_copy(out=CR[:, :, 1 + q, 1:33], in_=CS[:, :, q, :])
+
+            load_chunk(0)
+            load_chunk(1)
+            for row0, vec in ((0, ln2_g), (32, ln2_b)):
+                nc.sync.dma_start(
+                    out=g0b[row0 : row0 + 20, :].rearrange("j (y q) -> j y q", q=8),
+                    in_=vec.rearrange("(y j q) -> j y q", y=16, q=8),
+                )
+            load_chunk(2)
+            nc.sync.dma_start(out=b2bc[:], in_=b2.partition_broadcast(P))
+
+            def load_w(g5):
+                wraws[g5] = wpool.tile([P, 4, DIM], BF16, name="wraw")
+                for q in range(8):
+                    nc.sync.dma_start(out=wraws[g5][q:P:8, :, :], in_=wv[g5, q])
+
+            load_w(0)
+            load_w(1)
+
+            for i in range(11):
+                if i < 8:
+                    haar(i)
+                    if i + 3 < 8:
+                        load_chunk(i + 3)
+                if i == 2:
+                    nc.vector.tensor_copy(out=g0f[:], in_=g0b[:])
+                    gps = psx.tile([P, P], F32, name="gps", tag="misc")
+                    nc.tensor.transpose(gps[:], g0f[:], ident[:])
+                    nc.vector.tensor_copy(out=gb[:], in_=gps[:])
+                if i == 7:
+                    cs_flat = CS[:].rearrange("p k q x -> p (k q x)")
+                    pdn = psx.tile([P, 2, 4, 32], F32, name="pdn", tag="misc")
+                    pup = psx.tile([P, 2, 4, 32], F32, name="pup", tag="misc")
+                    nc.tensor.matmul(out=pdn[:].rearrange("p k q x -> p (k q x)"), lhsT=sh_dn[:], rhs=cs_flat, start=True, stop=True)
+                    nc.tensor.matmul(out=pup[:].rearrange("p k q x -> p (k q x)"), lhsT=sh_up[:], rhs=cs_flat, start=True, stop=True)
+                    nc.vector.tensor_copy(out=CR[:, :, 0, 1:33], in_=pdn[:, :, 3, :])
+                    nc.vector.tensor_copy(out=CR[:, :, 5, 1:33], in_=pup[:, :, 0, :])
+                if 1 <= i <= 8:
+                    turn_first(i - 1)
+                if 2 <= i <= 9:
+                    turn_second(i - 2)
+                if 1 <= i <= 5:
+                    wgrps[i - 1] = wpool.tile([P, DIM, 4], BF16, name="wgrp", align_bytes=64)
+                    nc.scalar.copy(out=wgrps[i - 1][:], in_=wraws[i - 1][:].rearrange("p t n -> p n t"))
+                    if i + 1 < 5:
+                        load_w(i + 1)
+                if 2 <= i <= 6:
+                    nc.vector.quantize_mx(
+                        out=wc[:, i - 2, :].bitcast(FP8X4),
+                        scales=ws[:, i - 2, :],
+                        in_=wgrps[i - 2][:].rearrange("p n t -> p (n t)"),
+                    )
+                if i >= 4 and i % 2 == 0:
+                    cell_sums(ORDER[i - 4] // 2)
+
+            nc.vector.tensor_tensor(out=A1[:], in0=CR[:, :, 0:5, :], in1=CR[:, :, 1:6, :], op=ALU.add)
+            nc.vector.tensor_tensor(out=Rw[:], in0=A1[:, :, 0:3:2, :], in1=A1[:, :, 2:5:2, :], op=ALU.add)
+            nc.vector.tensor_tensor(out=Bw[:], in0=Rw[:, :, :, 0:33], in1=Rw[:, :, :, 1:34], op=ALU.add)
+            nc.vector.tensor_tensor(out=Bc[:], in0=A1[:, :, 1:4:2, 0:33], in1=A1[:, :, 1:4:2, 1:34], op=ALU.add)
+            nc.vector.tensor_tensor(out=ST[:], in0=Bw[:, :, :, 0:31:2], in1=Bw[:, :, :, 2:33:2], op=ALU.add)
+            nc.vector.tensor_tensor(out=ST[:], in0=ST[:], in1=Bc[:, :, :, 1:32:2], op=ALU.add)
+            s1 = ST[:, 0, :, :].rearrange("p e j -> p (e j)")
+            s2 = ST[:, 1, :, :].rearrange("p e j -> p (e j)")
+            nc.vector.tensor_scalar(out=mean[:], in0=s1, scalar1=64.0 / KDIM, scalar2=None, op0=ALU.mult)
+            nc.vector.tensor_tensor(out=tmp[:], in0=mean[:], in1=mean[:], op=ALU.mult)
+            nc.vector.tensor_scalar(out=va[:], in0=s2, scalar1=1.0 / KDIM, scalar2=36.0e-5, op0=ALU.mult, op1=ALU.add)
+            nc.vector.tensor_tensor(out=va[:], in0=va[:], in1=tmp[:], op=ALU.subtract)
+            nc.scalar.sqrt(tmp[:], va[:])
+            nc.vector.reciprocal(rstd[:], tmp[:])
+            nc.vector.tensor_tensor(out=tmp[:], in0=rstd[:], in1=rstd[:], op=ALU.mult)
+            nc.vector.tensor_tensor(out=tmp[:], in0=tmp[:], in1=va[:], op=ALU.mult)
+            nc.vector.tensor_scalar(out=tmp[:], in0=tmp[:], scalar1=-0.5, scalar2=1.5, op0=ALU.mult, op1=ALU.add)
+            nc.vector.tensor_tensor(out=rstd[:], in0=rstd[:], in1=tmp[:], op=ALU.mult)
+            nc.vector.scalar_tensor_tensor(
+                out=nbias[:], in0=mean[:], scalar=-1.0, in1=rstd[:], op0=ALU.mult, op1=ALU.mult
+            )
+
+        with ExitStack() as pb:
+            npool = pb.enter_context(tc.tile_pool(name="npool", bufs=4))
+            zpool = pb.enter_context(tc.tile_pool(name="zpool", bufs=3))
+            cpool = pb.enter_context(tc.tile_pool(name="cpool", bufs=2))
+            iopool = pb.enter_context(tc.tile_pool(name="iopool", bufs=3))
+            pst = pb.enter_context(tc.psum_pool(name="pst", bufs=6))
+            psm = pb.enter_context(tc.psum_pool(name="psm", bufs=2))
+            pb.enter_context(tc.manual_schedule())
+
+            nbs = {}
+            tbs = {}
+            tks = {}
+            codes = {}
+            zis = {}
+
+            def load(r):
+                tks[r] = iopool.tile([P, 2, DIM], BF16, name="tk")
+                nc.sync.dma_start(out=tks[r][:], in_=tok_v[:, :, r, :])
+
+            def add_bias(r):
+                tb = iopool.tile([P, 2, DIM], F32, name="tb")
+                nc.vector.tensor_tensor(
+                    out=tb[:], in0=tks[r][:], in1=b2bc[:].unsqueeze(1).to_broadcast([P, 2, DIM]), op=ALU.add
+                )
+                tbs[r] = tb
+
+            def norm(r, slot):
+                e, s = divmod(slot, 5)
+                if s == 0:
+                    nbs[(r, e)] = npool.tile([P, KDIM], F32, name="nb")
+                nbv = nbs[(r, e)][:].rearrange("p (z s a h c) -> p s a h z c", z=4, s=5, a=8, h=2)
+                col = 16 * e + r
+                srcw = W[:, 8 * e + ROW0[s] : 8 * e + ROW0[s] + 8, 8 * r + COL0[s] : 8 * r + COL0[s] + 8, :].rearrange("p a (h z) c -> p a h z c", z=4)
+                if slot in S_SLOTS:
+                    nc.scalar.activation(
+                        out=nbv[:, s], in_=srcw, func=ACT.Identity,
+                        scale=rstd[:, col : col + 1], bias=nbias[:, col : col + 1],
+                    )
+                else:
+                    nc.vector.tensor_scalar(
+                        out=nbv[:, s], in0=srcw,
+                        scalar1=rstd[:, col : col + 1], scalar2=nbias[:, col : col + 1],
+                        op0=ALU.mult, op1=ALU.add,
+                    )
+
+            def quantise(r, g5):
+                zc, zs = codes[r]
+                nc.vector.quantize_mx(
+                    out=zc[:, g5, :].bitcast(FP8X4), scales=zs[:, g5, :],
+                    in_=zis[(r, g5)][:].rearrange("p c t -> p (c t)"),
+                )
+
+            def project(r):
+                zc, zs = codes[r]
+                ot = iopool.tile([P, 2, DIM], F32, name="ot")
+                accs = []
+                for u in range(2):
+                    acc = psm.tile([P, DIM], F32, name="acc")
+                    for g5 in range(5):
+                        nc.tensor.matmul_mx(
+                            out=acc[:],
+                            lhsT=zc[:, g5, P * u : P * u + P].bitcast(FP8X4),
+                            lhsT_scale=zs[:, g5, P * u : P * u + P],
+                            rhs=wc[:, g5, :].bitcast(FP8X4),
+                            rhs_scale=ws[:, g5, :],
+                            start=(g5 == 0),
+                            stop=(g5 == 4),
+                        )
+                    accs.append(acc)
+                for u in range(2):
+                    nc.vector.tensor_tensor(out=ot[:, u, :], in0=accs[u][:], in1=tbs[r][:, u, :], op=ALU.add)
+                nc.sync.dma_start(out=out_v[:, :, r, :], in_=ot[:])
+
+            load(0)
+            load(1)
+            for slot in range(10):
+                norm(0, slot)
+            add_bias(0)
+            for r in range(16):
+                if r + 2 < 16:
+                    load(r + 2)
+                zc_t = cpool.tile([P, 5, 256], U32, name="zc", align_bytes=64)
+                zs_t = cpool.tile([P, 5, 256], U8, name="zs", align_bytes=64)
+                codes[r] = (zc_t, zs_t)
+                for g5 in range(5):
+                    zp = zpool.tile([P, 4, 256], BF16, name="zp")
+                    for half in range(2):
+                        pt = pst.tile([P, 2, 2, P], F32, name="pt")
+                        for a in range(2):
+                            sl = 4 * g5 + 2 * half + a
+                            for u in range(2):
+                                nc.tensor.transpose(pt[:, a, u, :], nbs[(r, u)][:, P * sl : P * sl + P], ident[:])
+                        for a in range(2):
+                            sl = 4 * g5 + 2 * half + a
+                            nc.scalar.activation(
+                                out=zp[:, 2 * half + a, :], in_=pt[:, a, :, :].rearrange("p u r -> p (u r)"),
+                                func=ACT.Identity, scale=gb[:, sl : sl + 1], bias=gb[:, 32 + sl : 33 + sl],
+                            )
+                    if r + 1 < 16:
+                        norm(r + 1, 2 * g5)
+                        norm(r + 1, 2 * g5 + 1)
+                    zi = zpool.tile([P, 256, 4], BF16, name="zi", align_bytes=64)
+                    zis[(r, g5)] = zi
+                    nc.vector.tensor_copy(
+                        out=zi[:].rearrange("p (c i) t -> p c t i", i=4),
+                        in_=zp[:].rearrange("p t (c i) -> p c t i", i=4),
+                    )
+                    if g5 >= 1:
+                        quantise(r, g5 - 1)
+                quantise(r, 4)
+                if r + 1 < 16:
+                    add_bias(r + 1)
+                if r >= 1:
+                    project(r - 1)
+            project(15)

@@ -21,6 +21,8 @@ ROW0 = (4, 0, 0, 8, 8)
 COL0 = (4, 0, 8, 0, 8)
 S_SLOTS = (1, 5, 9)
 ORDER = (6, 7, 0, 1, 2, 3, 4, 5)
+VECTOR_TAP = (3, 0)
+EARLY = 3
 
 
 def tile_shiftedpatchtokenization_pb_t_kernel(tc, x, ln2_g, ln2_b, w2, b2, tok, out):
@@ -40,18 +42,19 @@ def tile_shiftedpatchtokenization_pb_t_kernel(tc, x, ln2_g, ln2_b, w2, b2, tok, 
         wc = keep.tile([P, 5, DIM], U32, align_bytes=64)
         ws = keep.tile([P, 5, DIM], U8, align_bytes=64)
         W = keep.tile([P, 24, 136, 8], F32)
-        CS = keep.tile([P, 2, 4, 32], F32)
+        bns = keep.tile([P, 4, 16, 6], F32)
+        sq_a = keep.tile([P, 32], F32)
         CR = keep.tile([P, 2, 6, 34], F32)
         A1 = keep.tile([P, 2, 5, 34], F32)
         Rw = keep.tile([P, 2, 2, 34], F32)
         Bw = keep.tile([P, 2, 2, 33], F32)
         Bc = keep.tile([P, 2, 2, 33], F32)
         ST = keep.tile([P, 2, 2, 16], F32)
-        mean = keep.tile([P, 32], F32)
-        va = keep.tile([P, 32], F32)
-        tmp = keep.tile([P, 32], F32)
-        rstd = keep.tile([P, 32], F32)
-        nbias = keep.tile([P, 32], F32)
+        mean = keep.tile([P, 2, 16], F32)
+        va = keep.tile([P, 2, 16], F32)
+        tmp = keep.tile([P, 2, 16], F32)
+        rstd = keep.tile([P, 2, 16], F32)
+        nbias = keep.tile([P, 2, 16], F32)
         one = keep.tile([P, 1], F32)
         mask_top = keep.tile([P, 1], F32)
         mask_bot = keep.tile([P, 1], F32)
@@ -76,14 +79,77 @@ def tile_shiftedpatchtokenization_pb_t_kernel(tc, x, ln2_g, ln2_b, w2, b2, tok, 
         nc.vector.memset(W[:, :, 0:4, :], 0.0)
         nc.vector.memset(W[:, :, 132:136, :], 0.0)
         nc.vector.memset(CR[:], 0.0)
-        nc.vector.memset(CS[:], 0.0)
+
+        wpool = ctx.enter_context(tc.tile_pool(name="wpool", bufs=1))
+        wraws = {}
+        wgrps = {}
+
+        def load_w(g5):
+            wraws[g5] = wpool.tile([P, 4, DIM], BF16, name="wraw", bufs=3)
+            for q in range(8):
+                nc.sync.dma_start(out=wraws[g5][q:P:8, :, :], in_=wv[g5, q])
+
+        def interleave_w(g5):
+            wgrps[g5] = wpool.tile([P, DIM, 4], BF16, name="wgrp", align_bytes=64, bufs=3)
+            nc.scalar.copy(out=wgrps[g5][:], in_=wraws[g5][:].rearrange("p t n -> p n t"))
+
+        def quantise_w(g5):
+            nc.vector.quantize_mx(
+                out=wc[:, g5, :].bitcast(FP8X4),
+                scales=ws[:, g5, :],
+                in_=wgrps[g5][:].rearrange("p n t -> p (n t)"),
+            )
+
+        def cell_stats(q, first, last):
+            r0 = 4 + 4 * q
+            for cx in range(first, last):
+                nc.vector.bn_stats(
+                    out=bns[:, q, cx, :],
+                    in_=W[:, r0 : r0 + 4, 4 + 8 * cx : 12 + 8 * cx, :].rearrange("p y (v x) c -> p y (x c) v", v=2),
+                )
+
+        def cell_sums(q, first, last):
+            cells = bns[:, q, first:last, :].rearrange("p a (v f) -> p (a v) f", v=2)
+            sums = CR[:, :, 1 + q, 1 + 2 * first : 1 + 2 * last]
+            sq = sq_a[:, 2 * first : 2 * last]
+            nc.vector.tensor_copy(out=sums[:, 0], in_=cells[:, :, 1])
+            nc.vector.tensor_tensor(out=sq, in0=cells[:, :, 1], in1=cells[:, :, 1], op=ALU.mult)
+            nc.vector.scalar_tensor_tensor(
+                out=sums[:, 1], in0=sq, scalar=128.0, in1=cells[:, :, 2], op0=ALU.mult, op1=ALU.add
+            )
+
+        def token_stats(j0, j1):
+            a, b = 2 * j0, 2 * j1 + 2
+            top = A1[:, :, 0:5, a:b]
+            nc.vector.tensor_tensor(out=top, in0=CR[:, :, 0:5, a:b], in1=CR[:, :, 1:6, a:b], op=ALU.add)
+            nc.vector.tensor_tensor(out=Rw[:, :, :, a:b], in0=A1[:, :, 0:3:2, a:b], in1=A1[:, :, 2:5:2, a:b], op=ALU.add)
+            nc.vector.tensor_tensor(
+                out=Bc[:, :, :, a : b - 1], in0=A1[:, :, 1:4:2, a : b - 1], in1=A1[:, :, 1:4:2, a + 1 : b], op=ALU.add
+            )
+            nc.vector.tensor_tensor(
+                out=Bw[:, :, :, a : b - 1], in0=Rw[:, :, :, a : b - 1], in1=Rw[:, :, :, a + 1 : b], op=ALU.add
+            )
+            st = ST[:, :, :, j0:j1]
+            nc.vector.tensor_tensor(
+                out=st, in0=Bw[:, :, :, a : b - 3 : 2], in1=Bw[:, :, :, a + 2 : b - 1 : 2], op=ALU.add
+            )
+            nc.vector.tensor_tensor(out=st, in0=st, in1=Bc[:, :, :, a + 1 : b - 2 : 2], op=ALU.add)
+            m, v, t, r, n = (z[:, :, j0:j1] for z in (mean, va, tmp, rstd, nbias))
+            nc.vector.tensor_scalar(out=m, in0=st[:, 0], scalar1=128.0 / KDIM, scalar2=None, op0=ALU.mult)
+            nc.vector.tensor_scalar(
+                out=v, in0=st[:, 1], scalar1=1.0 / KDIM, scalar2=36.0e-5, op0=ALU.mult, op1=ALU.add
+            )
+            nc.vector.tensor_tensor(out=t, in0=m, in1=m, op=ALU.mult)
+            nc.vector.tensor_tensor(out=v, in0=v, in1=t, op=ALU.subtract)
+            nc.scalar.sqrt(t, v)
+            nc.vector.reciprocal(r, t)
+            nc.vector.scalar_tensor_tensor(out=n, in0=m, scalar=-1.0, in1=r, op0=ALU.mult, op1=ALU.mult)
 
         with ExitStack() as pa:
             xpool = pa.enter_context(tc.tile_pool(name="xpool", bufs=3))
             hpool = pa.enter_context(tc.tile_pool(name="hpool", bufs=2))
             tpool = pa.enter_context(tc.tile_pool(name="tpool", bufs=1))
-            psa = pa.enter_context(tc.psum_pool(name="psa", bufs=3))
-            psx = pa.enter_context(tc.psum_pool(name="psx", bufs=2))
+            psa = pa.enter_context(tc.psum_pool(name="psa", bufs=4))
 
             m_a = tpool.tile([P, 2056], F32)
             m_b = tpool.tile([P, 2056], F32)
@@ -93,12 +159,6 @@ def tile_shiftedpatchtokenization_pb_t_kernel(tc, x, ln2_g, ln2_b, w2, b2, tok, 
             g0b = tpool.tile([P, P], BF16)
             g0f = tpool.tile([P, P], F32)
             nc.vector.memset(g0b[:], 0.0)
-            bns = tpool.tile([P, 4, 32, 6], F32)
-            sq_a = tpool.tile([P, 32], F32)
-            sq_b = tpool.tile([P, 32], F32)
-            wpool = pa.enter_context(tc.tile_pool(name="wpool", bufs=2))
-            wraws = {}
-            wgrps = {}
 
             pa.enter_context(tc.manual_schedule())
             xss = {}
@@ -106,40 +166,60 @@ def tile_shiftedpatchtokenization_pb_t_kernel(tc, x, ln2_g, ln2_b, w2, b2, tok, 
 
             def load_chunk(i):
                 xs = xpool.tile([P, 8, 1024], BF16, name="xs")
-                nc.sync.dma_start(out=xs[:], in_=xv[:, :, ORDER[i], :])
+                for hq in range(2):
+                    gs = slice(4 * hq, 4 * hq + 4)
+                    nc.sync.dma_start(out=xs[:, gs, :], in_=xv[:, gs, ORDER[i], :])
                 xss[i] = xs
 
+            def taps(i):
+                return xss[i][:].rearrange("p g (o e x f) -> p g o e x f", o=2, e=2, x=128, f=2)
+
             def haar(i):
-                xq = xss[i][:].rearrange("p g (o e x f) -> p g o e x f", o=2, e=2, x=128, f=2)
+                xq = taps(i)
                 h = hpool.tile([P, 8, 2, 128], F32, name="h")
-                nc.vector.scalar_tensor_tensor(
-                    out=h[:], in0=xq[:, :, :, 0, :, 0], scalar=3.0, in1=xq[:, :, :, 0, :, 1],
-                    op0=ALU.mult, op1=ALU.subtract,
-                )
-                nc.vector.tensor_tensor(out=h[:], in0=h[:], in1=xq[:, :, :, 1, :, 0], op=ALU.subtract)
+                for hq in range(2):
+                    gs = slice(4 * hq, 4 * hq + 4)
+                    nc.vector.scalar_tensor_tensor(
+                        out=h[:, gs], in0=xq[:, gs, :, 0, :, 0], scalar=3.0, in1=xq[:, gs, :, 0, :, 1],
+                        op0=ALU.mult, op1=ALU.subtract,
+                    )
+                    if (i, hq) == VECTOR_TAP:
+                        nc.vector.tensor_tensor(
+                            out=h[:, gs], in0=h[:, gs], in1=xq[:, gs, :, 1, :, 0], op=ALU.subtract
+                        )
                 hs[i] = h
+
+            def empty(k, i, out, in_):
+                if i == 7 and k % 2 == 1:
+                    nc.vector.tensor_copy(out=out, in_=in_)
+                else:
+                    nc.scalar.copy(out=out, in_=in_)
 
             def turn_first(i):
                 h = hs[i]
-                xq = xss[i][:].rearrange("p g (o e x f) -> p g o e x f", o=2, e=2, x=128, f=2)
+                xq = taps(i)
                 m_t = m_a if i % 2 == 0 else m_b
                 m_v = m_t[:, 4:2052].rearrange("p (c o b g) -> p c o b g", c=8, o=2, b=16)
-                for o in range(2):
-                    for hq in range(2):
+                for hq in range(2):
+                    p1s = []
+                    for o in range(2):
                         p1 = psa.tile([P, 4, P], F32, name="p1")
+                        p1s.append(p1)
                         for gq in range(4):
                             nc.tensor.matmul(
                                 out=p1[:, gq, :], lhsT=h[:, 4 * hq + gq, o, :], rhs=ident[:],
                                 is_transpose=True, start=(gq == 0), stop=False,
                             )
-                        for gq in range(4):
-                            nc.tensor.matmul(
-                                out=p1[:, gq, :], lhsT=xq[:, 4 * hq + gq, o, 1, :, 1], rhs=neg_id[:],
-                                start=False, stop=(gq == 3),
-                            )
-                        nc.scalar.copy(
-                            out=m_v[:, :, o, :, 4 * hq : 4 * hq + 4],
-                            in_=p1[:].rearrange("p q (b c) -> p c b q", c=8),
+                    for o in range(2):
+                        for tap in (1,) if (i, hq) == VECTOR_TAP else (0, 1):
+                            for gq in range(4):
+                                nc.tensor.matmul(
+                                    out=p1s[o][:, gq, :], lhsT=xq[:, 4 * hq + gq, o, 1, :, tap], rhs=neg_id[:],
+                                    start=False, stop=(tap == 1 and gq == 3),
+                                )
+                        empty(
+                            o, i, m_v[:, :, o, :, 4 * hq : 4 * hq + 4],
+                            p1s[o][:].rearrange("p q (b c) -> p c b q", c=8),
                         )
 
             def turn_second(i):
@@ -161,105 +241,73 @@ def tile_shiftedpatchtokenization_pb_t_kernel(tc, x, ln2_g, ln2_b, w2, b2, tok, 
                             dst = W[:, r, 4:132, 4 * ch : 4 * ch + 4]
                             srcv = p2[:].rearrange("p c x -> p x c")
                             if mask is None:
-                                nc.scalar.copy(out=dst, in_=srcv)
+                                empty(ch, i, dst, srcv)
                             else:
-                                nc.scalar.activation(out=dst, in_=srcv, func=ACT.Copy, scale=mask[:, 0:1])
+                                nc.vector.tensor_scalar(
+                                    out=dst, in0=srcv, scalar1=mask[:, 0:1], scalar2=None, op0=ALU.mult
+                                )
 
-            def cell_sums(q):
-                r0 = 4 + 4 * q
-                for cx in range(32):
-                    nc.vector.bn_stats(out=bns[:, q, cx, :], in_=W[:, r0 : r0 + 4, 4 + 4 * cx : 8 + 4 * cx, :])
-                nc.vector.tensor_tensor(out=CS[:, 0, q, :], in0=bns[:, q, :, 1], in1=bns[:, q, :, 4], op=ALU.add)
-                nc.vector.tensor_tensor(out=sq_a[:], in0=bns[:, q, :, 1], in1=bns[:, q, :, 1], op=ALU.mult)
-                nc.vector.tensor_tensor(out=sq_b[:], in0=bns[:, q, :, 4], in1=bns[:, q, :, 4], op=ALU.mult)
-                nc.vector.tensor_tensor(out=sq_a[:], in0=sq_a[:], in1=sq_b[:], op=ALU.add)
-                nc.vector.tensor_tensor(out=sq_b[:], in0=bns[:, q, :, 2], in1=bns[:, q, :, 5], op=ALU.add)
-                nc.vector.scalar_tensor_tensor(
-                    out=CS[:, 1, q, :], in0=sq_a[:], scalar=64.0, in1=sq_b[:], op0=ALU.mult, op1=ALU.add
-                )
-                nc.vector.tensor_copy(out=CR[:, :, 1 + q, 1:33], in_=CS[:, :, q, :])
 
             load_chunk(0)
+            load_w(0)
             load_chunk(1)
             for row0, vec in ((0, ln2_g), (32, ln2_b)):
                 nc.sync.dma_start(
                     out=g0b[row0 : row0 + 20, :].rearrange("j (y q) -> j y q", q=8),
                     in_=vec.rearrange("(y j q) -> j y q", y=16, q=8),
                 )
+            load_w(1)
             load_chunk(2)
             nc.sync.dma_start(out=b2bc[:], in_=b2.partition_broadcast(P))
-
-            def load_w(g5):
-                wraws[g5] = wpool.tile([P, 4, DIM], BF16, name="wraw")
-                for q in range(8):
-                    nc.sync.dma_start(out=wraws[g5][q:P:8, :, :], in_=wv[g5, q])
-
-            load_w(0)
-            load_w(1)
 
             for i in range(11):
                 if i < 8:
                     haar(i)
                     if i + 3 < 8:
                         load_chunk(i + 3)
-                if i == 2:
+                    if 5 <= i + 1 < 8:
+                        load_w(i - 2)
+                if i == 3:
                     nc.vector.tensor_copy(out=g0f[:], in_=g0b[:])
-                    gps = psx.tile([P, P], F32, name="gps", tag="misc")
-                    nc.tensor.transpose(gps[:], g0f[:], ident[:])
-                    nc.vector.tensor_copy(out=gb[:], in_=gps[:])
-                if i == 7:
-                    cs_flat = CS[:].rearrange("p k q x -> p (k q x)")
-                    pdn = psx.tile([P, 2, 4, 32], F32, name="pdn", tag="misc")
-                    pup = psx.tile([P, 2, 4, 32], F32, name="pup", tag="misc")
-                    nc.tensor.matmul(out=pdn[:].rearrange("p k q x -> p (k q x)"), lhsT=sh_dn[:], rhs=cs_flat, start=True, stop=True)
-                    nc.tensor.matmul(out=pup[:].rearrange("p k q x -> p (k q x)"), lhsT=sh_up[:], rhs=cs_flat, start=True, stop=True)
-                    nc.vector.tensor_copy(out=CR[:, :, 0, 1:33], in_=pdn[:, :, 3, :])
-                    nc.vector.tensor_copy(out=CR[:, :, 5, 1:33], in_=pup[:, :, 0, :])
+                    gps = psa.tile([P, 4, P], F32, name="p2")
+                    nc.tensor.transpose(gps[:, 0, :], g0f[:], ident[:])
+                    nc.vector.tensor_copy(out=gb[:], in_=gps[:, 0, :])
+                if i == 0:
+                    interleave_w(0)
                 if 1 <= i <= 8:
                     turn_first(i - 1)
+                if i == 1:
+                    interleave_w(1)
                 if 2 <= i <= 9:
                     turn_second(i - 2)
-                if 1 <= i <= 5:
-                    wgrps[i - 1] = wpool.tile([P, DIM, 4], BF16, name="wgrp", align_bytes=64)
-                    nc.scalar.copy(out=wgrps[i - 1][:], in_=wraws[i - 1][:].rearrange("p t n -> p n t"))
-                    if i + 1 < 5:
-                        load_w(i + 1)
-                if 2 <= i <= 6:
-                    nc.vector.quantize_mx(
-                        out=wc[:, i - 2, :].bitcast(FP8X4),
-                        scales=ws[:, i - 2, :],
-                        in_=wgrps[i - 2][:].rearrange("p n t -> p (n t)"),
-                    )
-                if i >= 4 and i % 2 == 0:
-                    cell_sums(ORDER[i - 4] // 2)
+                if i in (2, 3):
+                    quantise_w(i - 2)
+                if 4 <= i <= 9:
+                    q = ORDER[i - i % 2 - 4] // 2
+                    cell_stats(q, 8 * (i % 2), 8 * (i % 2) + 8)
+                    if i % 2 == 1:
+                        cell_sums(q, 0, 16)
+                if i == 9:
+                    moved = psa.tile([P, 2, 2, 32], F32, name="p1")
+                    for n, shifter, cell_row in ((0, sh_dn, 4), (1, sh_up, 1)):
+                        nc.tensor.matmul(
+                            out=moved[:, n], lhsT=shifter[:], rhs=CR[:, :, cell_row, 1:33], start=True, stop=True
+                        )
+                    nc.vector.tensor_copy(out=CR[:, :, 0, 1:33], in_=moved[:, 0])
+                    nc.vector.tensor_copy(out=CR[:, :, 5, 1:33], in_=moved[:, 1])
+                if i == 10:
+                    cell_stats(ORDER[6] // 2, 0, EARLY + 1)
+                    cell_sums(ORDER[6] // 2, 0, EARLY + 1)
+            for g5 in range(2, 5):
+                interleave_w(g5)
 
-            nc.vector.tensor_tensor(out=A1[:], in0=CR[:, :, 0:5, :], in1=CR[:, :, 1:6, :], op=ALU.add)
-            nc.vector.tensor_tensor(out=Rw[:], in0=A1[:, :, 0:3:2, :], in1=A1[:, :, 2:5:2, :], op=ALU.add)
-            nc.vector.tensor_tensor(out=Bw[:], in0=Rw[:, :, :, 0:33], in1=Rw[:, :, :, 1:34], op=ALU.add)
-            nc.vector.tensor_tensor(out=Bc[:], in0=A1[:, :, 1:4:2, 0:33], in1=A1[:, :, 1:4:2, 1:34], op=ALU.add)
-            nc.vector.tensor_tensor(out=ST[:], in0=Bw[:, :, :, 0:31:2], in1=Bw[:, :, :, 2:33:2], op=ALU.add)
-            nc.vector.tensor_tensor(out=ST[:], in0=ST[:], in1=Bc[:, :, :, 1:32:2], op=ALU.add)
-            s1 = ST[:, 0, :, :].rearrange("p e j -> p (e j)")
-            s2 = ST[:, 1, :, :].rearrange("p e j -> p (e j)")
-            nc.vector.tensor_scalar(out=mean[:], in0=s1, scalar1=64.0 / KDIM, scalar2=None, op0=ALU.mult)
-            nc.vector.tensor_tensor(out=tmp[:], in0=mean[:], in1=mean[:], op=ALU.mult)
-            nc.vector.tensor_scalar(out=va[:], in0=s2, scalar1=1.0 / KDIM, scalar2=36.0e-5, op0=ALU.mult, op1=ALU.add)
-            nc.vector.tensor_tensor(out=va[:], in0=va[:], in1=tmp[:], op=ALU.subtract)
-            nc.scalar.sqrt(tmp[:], va[:])
-            nc.vector.reciprocal(rstd[:], tmp[:])
-            nc.vector.tensor_tensor(out=tmp[:], in0=rstd[:], in1=rstd[:], op=ALU.mult)
-            nc.vector.tensor_tensor(out=tmp[:], in0=tmp[:], in1=va[:], op=ALU.mult)
-            nc.vector.tensor_scalar(out=tmp[:], in0=tmp[:], scalar1=-0.5, scalar2=1.5, op0=ALU.mult, op1=ALU.add)
-            nc.vector.tensor_tensor(out=rstd[:], in0=rstd[:], in1=tmp[:], op=ALU.mult)
-            nc.vector.scalar_tensor_tensor(
-                out=nbias[:], in0=mean[:], scalar=-1.0, in1=rstd[:], op0=ALU.mult, op1=ALU.mult
-            )
+            token_stats(0, EARLY)
 
         with ExitStack() as pb:
             npool = pb.enter_context(tc.tile_pool(name="npool", bufs=4))
             zpool = pb.enter_context(tc.tile_pool(name="zpool", bufs=3))
             cpool = pb.enter_context(tc.tile_pool(name="cpool", bufs=2))
-            iopool = pb.enter_context(tc.tile_pool(name="iopool", bufs=3))
+            iopool = pb.enter_context(tc.tile_pool(name="iopool", bufs=2))
             pst = pb.enter_context(tc.psum_pool(name="pst", bufs=6))
             psm = pb.enter_context(tc.psum_pool(name="psm", bufs=2))
             pb.enter_context(tc.manual_schedule())
@@ -271,7 +319,7 @@ def tile_shiftedpatchtokenization_pb_t_kernel(tc, x, ln2_g, ln2_b, w2, b2, tok, 
             zis = {}
 
             def load(r):
-                tks[r] = iopool.tile([P, 2, DIM], BF16, name="tk")
+                tks[r] = iopool.tile([P, 2, DIM], BF16, name="tk", bufs=3)
                 nc.sync.dma_start(out=tks[r][:], in_=tok_v[:, :, r, :])
 
             def add_bias(r):
@@ -286,17 +334,16 @@ def tile_shiftedpatchtokenization_pb_t_kernel(tc, x, ln2_g, ln2_b, w2, b2, tok, 
                 if s == 0:
                     nbs[(r, e)] = npool.tile([P, KDIM], F32, name="nb")
                 nbv = nbs[(r, e)][:].rearrange("p (z s a h c) -> p s a h z c", z=4, s=5, a=8, h=2)
-                col = 16 * e + r
                 srcw = W[:, 8 * e + ROW0[s] : 8 * e + ROW0[s] + 8, 8 * r + COL0[s] : 8 * r + COL0[s] + 8, :].rearrange("p a (h z) c -> p a h z c", z=4)
                 if slot in S_SLOTS:
                     nc.scalar.activation(
                         out=nbv[:, s], in_=srcw, func=ACT.Identity,
-                        scale=rstd[:, col : col + 1], bias=nbias[:, col : col + 1],
+                        scale=rstd[:, e, r : r + 1], bias=nbias[:, e, r : r + 1],
                     )
                 else:
                     nc.vector.tensor_scalar(
                         out=nbv[:, s], in0=srcw,
-                        scalar1=rstd[:, col : col + 1], scalar2=nbias[:, col : col + 1],
+                        scalar1=rstd[:, e, r : r + 1], scalar2=nbias[:, e, r : r + 1],
                         op0=ALU.mult, op1=ALU.add,
                     )
 
@@ -333,6 +380,8 @@ def tile_shiftedpatchtokenization_pb_t_kernel(tc, x, ln2_g, ln2_b, w2, b2, tok, 
             for slot in range(10):
                 norm(0, slot)
             add_bias(0)
+            cell_stats(ORDER[6] // 2, EARLY + 1, 16)
+            cell_sums(ORDER[6] // 2, EARLY + 1, 16)
             for r in range(16):
                 if r + 2 < 16:
                     load(r + 2)
@@ -362,11 +411,15 @@ def tile_shiftedpatchtokenization_pb_t_kernel(tc, x, ln2_g, ln2_b, w2, b2, tok, 
                         out=zi[:].rearrange("p (c i) t -> p c t i", i=4),
                         in_=zp[:].rearrange("p t (c i) -> p c t i", i=4),
                     )
+                    if r == 0 and g5 >= 2:
+                        quantise_w(g5)
                     if g5 >= 1:
                         quantise(r, g5 - 1)
                 quantise(r, 4)
-                if r + 1 < 16:
-                    add_bias(r + 1)
+                if r == 0:
+                    token_stats(EARLY, 16)
                 if r >= 1:
                     project(r - 1)
+                if r + 1 < 16:
+                    add_bias(r + 1)
             project(15)

@@ -21,7 +21,7 @@ ROW0 = (4, 0, 0, 8, 8)
 COL0 = (4, 0, 8, 0, 8)
 S_SLOTS = (1, 5, 9)
 ORDER = (6, 7, 0, 1, 2, 3, 4, 5)
-VECTOR_TAP = (3, 0)
+VECTOR_TAP = 6
 EARLY = 3
 
 
@@ -90,7 +90,7 @@ def tile_shiftedpatchtokenization_pb_t_kernel(tc, x, ln2_g, ln2_b, w2, b2, tok, 
                 nc.sync.dma_start(out=wraws[g5][q:P:8, :, :], in_=wv[g5, q])
 
         def interleave_w(g5):
-            wgrps[g5] = wpool.tile([P, DIM, 4], BF16, name="wgrp", align_bytes=64, bufs=3)
+            wgrps[g5] = wpool.tile([P, DIM, 4], BF16, name="wgrp", align_bytes=64, bufs=4)
             nc.scalar.copy(out=wgrps[g5][:], in_=wraws[g5][:].rearrange("p t n -> p n t"))
 
         def quantise_w(g5):
@@ -134,20 +134,25 @@ def tile_shiftedpatchtokenization_pb_t_kernel(tc, x, ln2_g, ln2_b, w2, b2, tok, 
                 out=st, in0=Bw[:, :, :, a : b - 3 : 2], in1=Bw[:, :, :, a + 2 : b - 1 : 2], op=ALU.add
             )
             nc.vector.tensor_tensor(out=st, in0=st, in1=Bc[:, :, :, a + 1 : b - 2 : 2], op=ALU.add)
-            m, v, t, r, n = (z[:, :, j0:j1] for z in (mean, va, tmp, rstd, nbias))
+            m, v, t = (z[:, :, j0:j1] for z in (mean, va, tmp))
             nc.vector.tensor_scalar(out=m, in0=st[:, 0], scalar1=128.0 / KDIM, scalar2=None, op0=ALU.mult)
             nc.vector.tensor_scalar(
                 out=v, in0=st[:, 1], scalar1=1.0 / KDIM, scalar2=36.0e-5, op0=ALU.mult, op1=ALU.add
             )
             nc.vector.tensor_tensor(out=t, in0=m, in1=m, op=ALU.mult)
             nc.vector.tensor_tensor(out=v, in0=v, in1=t, op=ALU.subtract)
-            nc.scalar.sqrt(t, v)
+
+        def token_root(j0, j1):
+            nc.scalar.sqrt(tmp[:, :, j0:j1], va[:, :, j0:j1])
+
+        def token_scale(j0, j1):
+            m, t, r, n = (z[:, :, j0:j1] for z in (mean, tmp, rstd, nbias))
             nc.vector.reciprocal(r, t)
             nc.vector.scalar_tensor_tensor(out=n, in0=m, scalar=-1.0, in1=r, op0=ALU.mult, op1=ALU.mult)
 
         with ExitStack() as pa:
-            xpool = pa.enter_context(tc.tile_pool(name="xpool", bufs=3))
-            hpool = pa.enter_context(tc.tile_pool(name="hpool", bufs=2))
+            xpool = pa.enter_context(tc.tile_pool(name="xpool", bufs=6))
+            hpool = pa.enter_context(tc.tile_pool(name="hpool", bufs=4))
             tpool = pa.enter_context(tc.tile_pool(name="tpool", bufs=1))
             psa = pa.enter_context(tc.psum_pool(name="psa", bufs=4))
 
@@ -164,130 +169,123 @@ def tile_shiftedpatchtokenization_pb_t_kernel(tc, x, ln2_g, ln2_b, w2, b2, tok, 
             xss = {}
             hs = {}
 
-            def load_chunk(i):
-                xs = xpool.tile([P, 8, 1024], BF16, name="xs")
-                for hq in range(2):
-                    gs = slice(4 * hq, 4 * hq + 4)
-                    nc.sync.dma_start(out=xs[:, gs, :], in_=xv[:, gs, ORDER[i], :])
-                xss[i] = xs
+            def load_half(k):
+                i, hq = divmod(k, 2)
+                xss[k] = xpool.tile([P, 4, 1024], BF16, name="xs")
+                nc.sync.dma_start(out=xss[k][:], in_=xv[:, 4 * hq : 4 * hq + 4, ORDER[i], :])
 
-            def taps(i):
-                return xss[i][:].rearrange("p g (o e x f) -> p g o e x f", o=2, e=2, x=128, f=2)
+            def taps(k):
+                return xss[k][:].rearrange("p g (o e x f) -> p g o e x f", o=2, e=2, x=128, f=2)
 
-            def haar(i):
-                xq = taps(i)
-                h = hpool.tile([P, 8, 2, 128], F32, name="h")
-                for hq in range(2):
-                    gs = slice(4 * hq, 4 * hq + 4)
-                    nc.vector.scalar_tensor_tensor(
-                        out=h[:, gs], in0=xq[:, gs, :, 0, :, 0], scalar=3.0, in1=xq[:, gs, :, 0, :, 1],
-                        op0=ALU.mult, op1=ALU.subtract,
-                    )
-                    if (i, hq) == VECTOR_TAP:
-                        nc.vector.tensor_tensor(
-                            out=h[:, gs], in0=h[:, gs], in1=xq[:, gs, :, 1, :, 0], op=ALU.subtract
-                        )
-                hs[i] = h
+            def haar(k):
+                xq = taps(k)
+                hs[k] = hpool.tile([P, 4, 2, 128], F32, name="h")
+                nc.vector.scalar_tensor_tensor(
+                    out=hs[k][:], in0=xq[:, :, :, 0, :, 0], scalar=3.0, in1=xq[:, :, :, 0, :, 1],
+                    op0=ALU.mult, op1=ALU.subtract,
+                )
+                if k == VECTOR_TAP:
+                    nc.vector.tensor_tensor(out=hs[k][:], in0=hs[k][:], in1=xq[:, :, :, 1, :, 0], op=ALU.subtract)
 
-            def empty(k, i, out, in_):
-                if i == 7 and k % 2 == 1:
+            def empty(n, i, out, in_):
+                if i == 7 and n % 2 == 1:
                     nc.vector.tensor_copy(out=out, in_=in_)
                 else:
                     nc.scalar.copy(out=out, in_=in_)
 
-            def turn_first(i):
-                h = hs[i]
-                xq = taps(i)
+            def turn_first(k):
+                i, hq = divmod(k, 2)
+                h = hs[k]
+                xq = taps(k)
                 m_t = m_a if i % 2 == 0 else m_b
                 m_v = m_t[:, 4:2052].rearrange("p (c o b g) -> p c o b g", c=8, o=2, b=16)
-                for hq in range(2):
-                    p1s = []
-                    for o in range(2):
-                        p1 = psa.tile([P, 4, P], F32, name="p1")
-                        p1s.append(p1)
+                p1s = []
+                for o in range(2):
+                    p1 = psa.tile([P, 4, P], F32, name="p1")
+                    p1s.append(p1)
+                    for gq in range(4):
+                        nc.tensor.matmul(
+                            out=p1[:, gq, :], lhsT=h[:, gq, o, :], rhs=ident[:],
+                            is_transpose=True, start=(gq == 0), stop=False,
+                        )
+                for o in range(2):
+                    for tap in (1,) if k == VECTOR_TAP else (0, 1):
                         for gq in range(4):
                             nc.tensor.matmul(
-                                out=p1[:, gq, :], lhsT=h[:, 4 * hq + gq, o, :], rhs=ident[:],
-                                is_transpose=True, start=(gq == 0), stop=False,
+                                out=p1s[o][:, gq, :], lhsT=xq[:, gq, o, 1, :, tap], rhs=neg_id[:],
+                                start=False, stop=(tap == 1 and gq == 3),
                             )
-                    for o in range(2):
-                        for tap in (1,) if (i, hq) == VECTOR_TAP else (0, 1):
-                            for gq in range(4):
-                                nc.tensor.matmul(
-                                    out=p1s[o][:, gq, :], lhsT=xq[:, 4 * hq + gq, o, 1, :, tap], rhs=neg_id[:],
-                                    start=False, stop=(tap == 1 and gq == 3),
-                                )
-                        empty(
-                            o, i, m_v[:, :, o, :, 4 * hq : 4 * hq + 4],
-                            p1s[o][:].rearrange("p q (b c) -> p c b q", c=8),
-                        )
+                    empty(
+                        o, i, m_v[:, :, o, :, 4 * hq : 4 * hq + 4],
+                        p1s[o][:].rearrange("p q (b c) -> p c b q", c=8),
+                    )
 
-            def turn_second(i):
-                u = ORDER[i]
+            def turn_second(k):
+                i, o = divmod(k, 2)
                 m_t = m_a if i % 2 == 0 else m_b
-                for o in range(2):
-                    ro = 2 * u + o
-                    jobs = [(4 + ro, 0, None)]
-                    if ro < 4:
-                        jobs.append((20 + ro, 1, mask_bot))
-                    if ro >= 12:
-                        jobs.append((ro - 12, -1, mask_top))
-                    for r, shift, mask in jobs:
-                        for ch in range(2):
-                            p2 = psa.tile([P, 4, P], F32, name="p2")
-                            for c4 in range(4):
-                                base = 4 + ((4 * ch + c4) * 2 + o) * P + shift
-                                nc.tensor.transpose(p2[:, c4, :], m_t[:, base : base + P], ident[:])
-                            dst = W[:, r, 4:132, 4 * ch : 4 * ch + 4]
-                            srcv = p2[:].rearrange("p c x -> p x c")
-                            if mask is None:
-                                empty(ch, i, dst, srcv)
-                            else:
-                                nc.vector.tensor_scalar(
-                                    out=dst, in0=srcv, scalar1=mask[:, 0:1], scalar2=None, op0=ALU.mult
-                                )
+                ro = 2 * ORDER[i] + o
+                jobs = [(4 + ro, 0, None)]
+                if ro < 4:
+                    jobs.append((20 + ro, 1, mask_bot))
+                if ro >= 12:
+                    jobs.append((ro - 12, -1, mask_top))
+                for r, shift, mask in jobs:
+                    for ch in range(2):
+                        p2 = psa.tile([P, 4, P], F32, name="p2")
+                        for c4 in range(4):
+                            base = 4 + ((4 * ch + c4) * 2 + o) * P + shift
+                            nc.tensor.transpose(p2[:, c4, :], m_t[:, base : base + P], ident[:])
+                        dst = W[:, r, 4:132, 4 * ch : 4 * ch + 4]
+                        srcv = p2[:].rearrange("p c x -> p x c")
+                        if mask is None:
+                            empty(ch, i, dst, srcv)
+                        else:
+                            nc.vector.tensor_scalar(
+                                out=dst, in0=srcv, scalar1=mask[:, 0:1], scalar2=None, op0=ALU.mult
+                            )
 
-
-            load_chunk(0)
+            load_half(0)
+            load_half(1)
             load_w(0)
-            load_chunk(1)
+            load_half(2)
+            load_half(3)
             for row0, vec in ((0, ln2_g), (32, ln2_b)):
                 nc.sync.dma_start(
                     out=g0b[row0 : row0 + 20, :].rearrange("j (y q) -> j y q", q=8),
                     in_=vec.rearrange("(y j q) -> j y q", y=16, q=8),
                 )
-            load_w(1)
-            load_chunk(2)
+            load_half(4)
+            load_half(5)
             nc.sync.dma_start(out=b2bc[:], in_=b2.partition_broadcast(P))
 
-            for i in range(11):
-                if i < 8:
-                    haar(i)
-                    if i + 3 < 8:
-                        load_chunk(i + 3)
-                    if 5 <= i + 1 < 8:
-                        load_w(i - 2)
-                if i == 3:
+            for k in range(20):
+                if k < 16:
+                    haar(k)
+                if k >= 2 and k - 2 < 16:
+                    turn_first(k - 2)
+                if 6 <= k + 4 < 16 and k >= 2:
+                    load_half(k + 4)
+                if k in (8, 11, 12, 13):
+                    load_w(max(1, k - 9))
+                if k == 1:
+                    interleave_w(0)
+                if k == 4:
                     nc.vector.tensor_copy(out=g0f[:], in_=g0b[:])
+                if k >= 4:
+                    turn_second(k - 4)
+                if k == 5:
+                    quantise_w(0)
+                if k == 7:
                     gps = psa.tile([P, 4, P], F32, name="p2")
                     nc.tensor.transpose(gps[:, 0, :], g0f[:], ident[:])
-                    nc.vector.tensor_copy(out=gb[:], in_=gps[:, 0, :])
-                if i == 0:
-                    interleave_w(0)
-                if 1 <= i <= 8:
-                    turn_first(i - 1)
-                if i == 1:
-                    interleave_w(1)
-                if 2 <= i <= 9:
-                    turn_second(i - 2)
-                if i in (2, 3):
-                    quantise_w(i - 2)
-                if 4 <= i <= 9:
-                    q = ORDER[i - i % 2 - 4] // 2
-                    cell_stats(q, 8 * (i % 2), 8 * (i % 2) + 8)
-                    if i % 2 == 1:
+                    nc.scalar.copy(out=gb[:], in_=gps[:, 0, :])
+                if k >= 8:
+                    q, part = divmod(k - 8, 4)
+                    q = ORDER[2 * q] // 2
+                    cell_stats(q, 4 * part, 4 * part + 4)
+                    if part == 3:
                         cell_sums(q, 0, 16)
-                if i == 9:
+                if k == 17:
                     moved = psa.tile([P, 2, 2, 32], F32, name="p1")
                     for n, shifter, cell_row in ((0, sh_dn, 4), (1, sh_up, 1)):
                         nc.tensor.matmul(
@@ -295,13 +293,14 @@ def tile_shiftedpatchtokenization_pb_t_kernel(tc, x, ln2_g, ln2_b, w2, b2, tok, 
                         )
                     nc.vector.tensor_copy(out=CR[:, :, 0, 1:33], in_=moved[:, 0])
                     nc.vector.tensor_copy(out=CR[:, :, 5, 1:33], in_=moved[:, 1])
-                if i == 10:
-                    cell_stats(ORDER[6] // 2, 0, EARLY + 1)
-                    cell_sums(ORDER[6] // 2, 0, EARLY + 1)
-            for g5 in range(2, 5):
+            cell_stats(ORDER[6] // 2, 0, EARLY + 1)
+            cell_sums(ORDER[6] // 2, 0, EARLY + 1)
+            for g5 in range(1, 4):
                 interleave_w(g5)
-
             token_stats(0, EARLY)
+            token_root(0, EARLY)
+            interleave_w(4)
+            token_scale(0, EARLY)
 
         with ExitStack() as pb:
             npool = pb.enter_context(tc.tile_pool(name="npool", bufs=4))
@@ -317,13 +316,14 @@ def tile_shiftedpatchtokenization_pb_t_kernel(tc, x, ln2_g, ln2_b, w2, b2, tok, 
             tks = {}
             codes = {}
             zis = {}
+            accs = {}
 
             def load(r):
                 tks[r] = iopool.tile([P, 2, DIM], BF16, name="tk", bufs=3)
                 nc.sync.dma_start(out=tks[r][:], in_=tok_v[:, :, r, :])
 
             def add_bias(r):
-                tb = iopool.tile([P, 2, DIM], F32, name="tb")
+                tb = iopool.tile([P, 2, DIM], F32, name="tb", bufs=3)
                 nc.vector.tensor_tensor(
                     out=tb[:], in0=tks[r][:], in1=b2bc[:].unsqueeze(1).to_broadcast([P, 2, DIM]), op=ALU.add
                 )
@@ -335,7 +335,7 @@ def tile_shiftedpatchtokenization_pb_t_kernel(tc, x, ln2_g, ln2_b, w2, b2, tok, 
                     nbs[(r, e)] = npool.tile([P, KDIM], F32, name="nb")
                 nbv = nbs[(r, e)][:].rearrange("p (z s a h c) -> p s a h z c", z=4, s=5, a=8, h=2)
                 srcw = W[:, 8 * e + ROW0[s] : 8 * e + ROW0[s] + 8, 8 * r + COL0[s] : 8 * r + COL0[s] + 8, :].rearrange("p a (h z) c -> p a h z c", z=4)
-                if slot in S_SLOTS:
+                if slot in S_SLOTS and r > 0:
                     nc.scalar.activation(
                         out=nbv[:, s], in_=srcw, func=ACT.Identity,
                         scale=rstd[:, e, r : r + 1], bias=nbias[:, e, r : r + 1],
@@ -354,34 +354,42 @@ def tile_shiftedpatchtokenization_pb_t_kernel(tc, x, ln2_g, ln2_b, w2, b2, tok, 
                     in_=zis[(r, g5)][:].rearrange("p c t -> p (c t)"),
                 )
 
-            def project(r):
+            def multiply(r, g5, us=(0, 1)):
                 zc, zs = codes[r]
-                ot = iopool.tile([P, 2, DIM], F32, name="ot")
-                accs = []
+                for u in us:
+                    if g5 == 0:
+                        acc = psm.tile([P, DIM], F32, name="acc")
+                        accs[(r, u)] = acc
+                    nc.tensor.matmul_mx(
+                        out=accs[(r, u)][:],
+                        lhsT=zc[:, g5, P * u : P * u + P].bitcast(FP8X4),
+                        lhsT_scale=zs[:, g5, P * u : P * u + P],
+                        rhs=wc[:, g5, :].bitcast(FP8X4),
+                        rhs_scale=ws[:, g5, :],
+                        start=(g5 == 0),
+                        stop=(g5 == 4),
+                    )
+
+            def finish(r):
+                tb = tbs[r]
                 for u in range(2):
-                    acc = psm.tile([P, DIM], F32, name="acc")
+                    nc.vector.tensor_tensor(out=tb[:, u, :], in0=accs[(r, u)][:], in1=tb[:, u, :], op=ALU.add)
+                    if r == 15:
+                        nc.sync.dma_start(out=out_v[:, u, r, :], in_=tb[:, u, :])
+                if r < 15:
+                    nc.sync.dma_start(out=out_v[:, :, r, :], in_=tb[:])
+
+            def project(r):
+                for u in range(2):
                     for g5 in range(5):
-                        nc.tensor.matmul_mx(
-                            out=acc[:],
-                            lhsT=zc[:, g5, P * u : P * u + P].bitcast(FP8X4),
-                            lhsT_scale=zs[:, g5, P * u : P * u + P],
-                            rhs=wc[:, g5, :].bitcast(FP8X4),
-                            rhs_scale=ws[:, g5, :],
-                            start=(g5 == 0),
-                            stop=(g5 == 4),
-                        )
-                    accs.append(acc)
-                for u in range(2):
-                    nc.vector.tensor_tensor(out=ot[:, u, :], in0=accs[u][:], in1=tbs[r][:, u, :], op=ALU.add)
-                nc.sync.dma_start(out=out_v[:, :, r, :], in_=ot[:])
+                        multiply(r, g5, (u,))
+                finish(r)
 
             load(0)
             load(1)
             for slot in range(10):
                 norm(0, slot)
             add_bias(0)
-            cell_stats(ORDER[6] // 2, EARLY + 1, 16)
-            cell_sums(ORDER[6] // 2, EARLY + 1, 16)
             for r in range(16):
                 if r + 2 < 16:
                     load(r + 2)
@@ -411,15 +419,29 @@ def tile_shiftedpatchtokenization_pb_t_kernel(tc, x, ln2_g, ln2_b, w2, b2, tok, 
                         out=zi[:].rearrange("p (c i) t -> p c t i", i=4),
                         in_=zp[:].rearrange("p t (c i) -> p c t i", i=4),
                     )
-                    if r == 0 and g5 >= 2:
+                    if r == 0 and g5 >= 1:
                         quantise_w(g5)
                     if g5 >= 1:
                         quantise(r, g5 - 1)
+                    if r == 0 and g5 < 4:
+                        cell_stats(ORDER[6] // 2, EARLY + 1 + 3 * g5, EARLY + 4 + 3 * g5)
+                    if r == 0 and g5 == 4:
+                        cell_sums(ORDER[6] // 2, EARLY + 1, 16)
+                    if r == 1 and g5 == 0:
+                        token_stats(EARLY, 16)
+                    if r == 1 and g5 == 2:
+                        token_root(EARLY, 16)
+                    if r == 1 and g5 == 3:
+                        token_scale(EARLY, 16)
+                    if r == 15 and g5 == 0:
+                        project(14)
+                    if r == 15 and g5 >= 2:
+                        multiply(15, g5 - 2)
                 quantise(r, 4)
-                if r == 0:
-                    token_stats(EARLY, 16)
-                if r >= 1:
+                if 1 <= r < 15:
                     project(r - 1)
                 if r + 1 < 16:
                     add_bias(r + 1)
-            project(15)
+            multiply(15, 3)
+            multiply(15, 4)
+            finish(15)

@@ -19,16 +19,16 @@ FLOPS = 2 * 4096 * KDIM * DIM
 
 ROW0 = (4, 0, 0, 8, 8)
 COL0 = (4, 0, 8, 0, 8)
-S_SLOTS = (1, 5, 9)
+S_SLOTS = (1, 5, 7, 9)
 ORDER = (6, 7, 0, 1, 2, 3, 4, 5)
-VECTOR_TAP = 6
+VECTOR_TAPS = (3, 6, 9, 12)
 EARLY = 3
 
 
 def tile_shiftedpatchtokenization_pb_t_kernel(tc, x, ln2_g, ln2_b, w2, b2, tok, out):
     nc = tc.nc
     xv = x.rearrange("b c (g u r) w -> (b c) g u (r w)", g=8, u=8)
-    wv = w2.rearrange("(y g t q) n -> g q y t n", y=16, g=5, t=4)
+    wv = w2.rearrange("(y j q) n -> q y j n", y=16, q=8)
     tok_v = tok.rearrange("b (g e j) d -> (b g) e j d", g=8, e=2)
     out_v = out.rearrange("b (g e j) d -> (b g) e j d", g=8, e=2)
 
@@ -50,8 +50,9 @@ def tile_shiftedpatchtokenization_pb_t_kernel(tc, x, ln2_g, ln2_b, w2, b2, tok, 
         Bw = keep.tile([P, 2, 2, 33], F32)
         Bc = keep.tile([P, 2, 2, 33], F32)
         ST = keep.tile([P, 2, 2, 16], F32)
-        mean = keep.tile([P, 2, 16], F32)
-        va = keep.tile([P, 2, 16], F32)
+        D3 = keep.tile([P, 2, 33], F32)
+        F3 = keep.tile([P, 2, 16], F32)
+        G3 = keep.tile([P, 2, 16], F32)
         tmp = keep.tile([P, 2, 16], F32)
         rstd = keep.tile([P, 2, 16], F32)
         nbias = keep.tile([P, 2, 16], F32)
@@ -84,14 +85,10 @@ def tile_shiftedpatchtokenization_pb_t_kernel(tc, x, ln2_g, ln2_b, w2, b2, tok, 
         wraws = {}
         wgrps = {}
 
-        def load_w(g5):
-            wraws[g5] = wpool.tile([P, 4, DIM], BF16, name="wraw", bufs=3)
-            for q in range(8):
-                nc.sync.dma_start(out=wraws[g5][q:P:8, :, :], in_=wv[g5, q])
-
         def interleave_w(g5):
             wgrps[g5] = wpool.tile([P, DIM, 4], BF16, name="wgrp", align_bytes=64, bufs=4)
-            nc.scalar.copy(out=wgrps[g5][:], in_=wraws[g5][:].rearrange("p t n -> p n t"))
+            raw = wraws[g5 // 2][:, 2 * (g5 % 2) : 2 * (g5 % 2) + 2, :]
+            nc.scalar.copy(out=wgrps[g5][:], in_=raw.rearrange("p a (b n) -> p n (a b)", n=DIM))
 
         def quantise_w(g5):
             nc.vector.quantize_mx(
@@ -112,46 +109,55 @@ def tile_shiftedpatchtokenization_pb_t_kernel(tc, x, ln2_g, ln2_b, w2, b2, tok, 
             cells = bns[:, q, first:last, :].rearrange("p a (v f) -> p (a v) f", v=2)
             sums = CR[:, :, 1 + q, 1 + 2 * first : 1 + 2 * last]
             sq = sq_a[:, 2 * first : 2 * last]
-            nc.vector.tensor_copy(out=sums[:, 0], in_=cells[:, :, 1])
-            nc.vector.tensor_tensor(out=sq, in0=cells[:, :, 1], in1=cells[:, :, 1], op=ALU.mult)
-            nc.vector.scalar_tensor_tensor(
-                out=sums[:, 1], in0=sq, scalar=128.0, in1=cells[:, :, 2], op0=ALU.mult, op1=ALU.add
-            )
+            return [
+                lambda: nc.vector.scalar_tensor_tensor(
+                    out=sq, in0=cells[:, :, 1], scalar=128.0 / KDIM, in1=cells[:, :, 1], op0=ALU.mult, op1=ALU.mult
+                ),
+                lambda: nc.vector.tensor_copy(out=sums[:, 0], in_=cells[:, :, 1]),
+                lambda: nc.vector.scalar_tensor_tensor(
+                    out=sums[:, 1], in0=cells[:, :, 2], scalar=1.0 / KDIM, in1=sq, op0=ALU.mult, op1=ALU.add
+                ),
+            ]
 
-        def token_stats(j0, j1):
+        def first_sums():
+            nc.vector.tensor_tensor(out=A1[:], in0=CR[:, :, 0:5, :], in1=CR[:, :, 1:6, :], op=ALU.add)
+            nc.vector.tensor_tensor(out=Rw[:], in0=A1[:, :, 0:3:2, :], in1=A1[:, :, 2:5:2, :], op=ALU.add)
+            nc.vector.tensor_tensor(out=Bc[:], in0=A1[:, :, 1:4:2, 0:33], in1=A1[:, :, 1:4:2, 1:34], op=ALU.add)
+            nc.vector.tensor_tensor(out=Bw[:], in0=Rw[:, :, :, 0:33], in1=Rw[:, :, :, 1:34], op=ALU.add)
+            nc.vector.tensor_tensor(out=ST[:], in0=Bw[:, :, :, 0:31:2], in1=Bw[:, :, :, 2:33:2], op=ALU.add)
+            nc.vector.tensor_tensor(out=ST[:], in0=ST[:], in1=Bc[:, :, :, 1:32:2], op=ALU.add)
+            nc.vector.tensor_scalar(out=ST[:, 1], in0=ST[:, 1], scalar1=36.0e-5, scalar2=None, op0=ALU.add)
+
+        def last_sums(j0, j1):
             a, b = 2 * j0, 2 * j1 + 2
-            top = A1[:, :, 0:5, a:b]
-            nc.vector.tensor_tensor(out=top, in0=CR[:, :, 0:5, a:b], in1=CR[:, :, 1:6, a:b], op=ALU.add)
-            nc.vector.tensor_tensor(out=Rw[:, :, :, a:b], in0=A1[:, :, 0:3:2, a:b], in1=A1[:, :, 2:5:2, a:b], op=ALU.add)
-            nc.vector.tensor_tensor(
-                out=Bc[:, :, :, a : b - 1], in0=A1[:, :, 1:4:2, a : b - 1], in1=A1[:, :, 1:4:2, a + 1 : b], op=ALU.add
-            )
-            nc.vector.tensor_tensor(
-                out=Bw[:, :, :, a : b - 1], in0=Rw[:, :, :, a : b - 1], in1=Rw[:, :, :, a + 1 : b], op=ALU.add
-            )
+            row, pair, four, six = CR[:, :, 3, :], D3[:, :, a : b - 1], F3[:, :, j0:j1], G3[:, :, j0:j1]
             st = ST[:, :, :, j0:j1]
-            nc.vector.tensor_tensor(
-                out=st, in0=Bw[:, :, :, a : b - 3 : 2], in1=Bw[:, :, :, a + 2 : b - 1 : 2], op=ALU.add
-            )
-            nc.vector.tensor_tensor(out=st, in0=st, in1=Bc[:, :, :, a + 1 : b - 2 : 2], op=ALU.add)
-            m, v, t = (z[:, :, j0:j1] for z in (mean, va, tmp))
-            nc.vector.tensor_scalar(out=m, in0=st[:, 0], scalar1=128.0 / KDIM, scalar2=None, op0=ALU.mult)
-            nc.vector.tensor_scalar(
-                out=v, in0=st[:, 1], scalar1=1.0 / KDIM, scalar2=36.0e-5, op0=ALU.mult, op1=ALU.add
-            )
-            nc.vector.tensor_tensor(out=t, in0=m, in1=m, op=ALU.mult)
-            nc.vector.tensor_tensor(out=v, in0=v, in1=t, op=ALU.subtract)
+            t, r, n = (z[:, :, j0:j1] for z in (tmp, rstd, nbias))
+            c = 128.0 / KDIM
 
-        def token_root(j0, j1):
-            nc.scalar.sqrt(tmp[:, :, j0:j1], va[:, :, j0:j1])
+            def add(out, in0, in1):
+                return lambda: nc.vector.tensor_tensor(out=out, in0=in0, in1=in1, op=ALU.add)
 
-        def token_scale(j0, j1):
-            m, t, r, n = (z[:, :, j0:j1] for z in (mean, tmp, rstd, nbias))
-            nc.vector.reciprocal(r, t)
-            nc.vector.scalar_tensor_tensor(out=n, in0=m, scalar=-1.0, in1=r, op0=ALU.mult, op1=ALU.mult)
+            def product(out, in0, scalar, in1):
+                return lambda: nc.vector.scalar_tensor_tensor(
+                    out=out, in0=in0, scalar=scalar, in1=in1, op0=ALU.mult, op1=ALU.mult
+                )
+
+            return [
+                add(pair, row[:, :, a : b - 1], row[:, :, a + 1 : b]),
+                add(four, D3[:, :, a : b - 3 : 2], D3[:, :, a + 2 : b - 1 : 2]),
+                add(six, four, D3[:, :, a + 1 : b - 2 : 2]),
+                add(st[:, :, 0], st[:, :, 0], four),
+                add(st[:, :, 1], st[:, :, 1], six),
+                product(t, st[:, 0], -c * c, st[:, 0]),
+                add(t, t, st[:, 1]),
+                lambda: nc.scalar.sqrt(t, t),
+                lambda: nc.vector.reciprocal(r, t),
+                product(n, st[:, 0], -c, r),
+            ]
 
         with ExitStack() as pa:
-            xpool = pa.enter_context(tc.tile_pool(name="xpool", bufs=6))
+            xpool = pa.enter_context(tc.tile_pool(name="xpool", bufs=7))
             hpool = pa.enter_context(tc.tile_pool(name="hpool", bufs=4))
             tpool = pa.enter_context(tc.tile_pool(name="tpool", bufs=1))
             psa = pa.enter_context(tc.psum_pool(name="psa", bufs=4))
@@ -174,6 +180,15 @@ def tile_shiftedpatchtokenization_pb_t_kernel(tc, x, ln2_g, ln2_b, w2, b2, tok, 
                 xss[k] = xpool.tile([P, 4, 1024], BF16, name="xs")
                 nc.sync.dma_start(out=xss[k][:], in_=xv[:, 4 * hq : 4 * hq + 4, ORDER[i], :])
 
+            def load_w(m):
+                wraws[m] = xpool.tile([P, 4, 1024], BF16, name="xs")
+                slots = min(8, 20 - 8 * m)
+                for q in range(8):
+                    nc.sync.dma_start(
+                        out=wraws[m][q:P:8, 0 : slots // 2, :].rearrange("y a (b n) -> y (a b) n", n=DIM),
+                        in_=wv[q, :, 8 * m : 8 * m + slots, :],
+                    )
+
             def taps(k):
                 return xss[k][:].rearrange("p g (o e x f) -> p g o e x f", o=2, e=2, x=128, f=2)
 
@@ -184,7 +199,7 @@ def tile_shiftedpatchtokenization_pb_t_kernel(tc, x, ln2_g, ln2_b, w2, b2, tok, 
                     out=hs[k][:], in0=xq[:, :, :, 0, :, 0], scalar=3.0, in1=xq[:, :, :, 0, :, 1],
                     op0=ALU.mult, op1=ALU.subtract,
                 )
-                if k == VECTOR_TAP:
+                if k in VECTOR_TAPS:
                     nc.vector.tensor_tensor(out=hs[k][:], in0=hs[k][:], in1=xq[:, :, :, 1, :, 0], op=ALU.subtract)
 
             def empty(n, i, out, in_):
@@ -209,7 +224,7 @@ def tile_shiftedpatchtokenization_pb_t_kernel(tc, x, ln2_g, ln2_b, w2, b2, tok, 
                             is_transpose=True, start=(gq == 0), stop=False,
                         )
                 for o in range(2):
-                    for tap in (1,) if k == VECTOR_TAP else (0, 1):
+                    for tap in (1,) if k in VECTOR_TAPS else (0, 1):
                         for gq in range(4):
                             nc.tensor.matmul(
                                 out=p1s[o][:, gq, :], lhsT=xq[:, gq, o, 1, :, tap], rhs=neg_id[:],
@@ -239,6 +254,8 @@ def tile_shiftedpatchtokenization_pb_t_kernel(tc, x, ln2_g, ln2_b, w2, b2, tok, 
                         srcv = p2[:].rearrange("p c x -> p x c")
                         if mask is None:
                             empty(ch, i, dst, srcv)
+                        elif ch == 0:
+                            nc.scalar.activation(out=dst, in_=srcv, func=ACT.Copy, scale=mask[:, 0:1])
                         else:
                             nc.vector.tensor_scalar(
                                 out=dst, in0=srcv, scalar1=mask[:, 0:1], scalar2=None, op0=ALU.mult
@@ -246,7 +263,6 @@ def tile_shiftedpatchtokenization_pb_t_kernel(tc, x, ln2_g, ln2_b, w2, b2, tok, 
 
             load_half(0)
             load_half(1)
-            load_w(0)
             load_half(2)
             load_half(3)
             for row0, vec in ((0, ln2_g), (32, ln2_b)):
@@ -256,35 +272,35 @@ def tile_shiftedpatchtokenization_pb_t_kernel(tc, x, ln2_g, ln2_b, w2, b2, tok, 
                 )
             load_half(4)
             load_half(5)
+            load_half(6)
             nc.sync.dma_start(out=b2bc[:], in_=b2.partition_broadcast(P))
 
             for k in range(20):
-                if k < 16:
-                    haar(k)
-                if k >= 2 and k - 2 < 16:
-                    turn_first(k - 2)
-                if 6 <= k + 4 < 16 and k >= 2:
-                    load_half(k + 4)
-                if k in (8, 11, 12, 13):
-                    load_w(max(1, k - 9))
-                if k == 1:
-                    interleave_w(0)
-                if k == 4:
-                    nc.vector.tensor_copy(out=g0f[:], in_=g0b[:])
-                if k >= 4:
-                    turn_second(k - 4)
-                if k == 5:
-                    quantise_w(0)
-                if k == 7:
-                    gps = psa.tile([P, 4, P], F32, name="p2")
-                    nc.tensor.transpose(gps[:, 0, :], g0f[:], ident[:])
-                    nc.scalar.copy(out=gb[:], in_=gps[:, 0, :])
                 if k >= 8:
                     q, part = divmod(k - 8, 4)
                     q = ORDER[2 * q] // 2
                     cell_stats(q, 4 * part, 4 * part + 4)
                     if part == 3:
-                        cell_sums(q, 0, 16)
+                        for op in cell_sums(q, 0, 16):
+                            op()
+                if k == 19:
+                    first_sums()
+                if k < 16:
+                    haar(k)
+                if k >= 2 and k - 2 < 16:
+                    turn_first(k - 2)
+                if 2 <= k <= 10:
+                    load_half(k + 5)
+                if 11 <= k <= 13:
+                    load_w(k - 11)
+                if k == 4:
+                    nc.vector.tensor_copy(out=g0f[:], in_=g0b[:])
+                if k >= 4:
+                    turn_second(k - 4)
+                if k == 7:
+                    gps = psa.tile([P, 4, P], F32, name="p2")
+                    nc.tensor.transpose(gps[:, 0, :], g0f[:], ident[:])
+                    nc.scalar.copy(out=gb[:], in_=gps[:, 0, :])
                 if k == 17:
                     moved = psa.tile([P, 2, 2, 32], F32, name="p1")
                     for n, shifter, cell_row in ((0, sh_dn, 4), (1, sh_up, 1)):
@@ -293,20 +309,23 @@ def tile_shiftedpatchtokenization_pb_t_kernel(tc, x, ln2_g, ln2_b, w2, b2, tok, 
                         )
                     nc.vector.tensor_copy(out=CR[:, :, 0, 1:33], in_=moved[:, 0])
                     nc.vector.tensor_copy(out=CR[:, :, 5, 1:33], in_=moved[:, 1])
-            cell_stats(ORDER[6] // 2, 0, EARLY + 1)
-            cell_sums(ORDER[6] // 2, 0, EARLY + 1)
-            for g5 in range(1, 4):
+            for g5 in range(4):
                 interleave_w(g5)
-            token_stats(0, EARLY)
-            token_root(0, EARLY)
+            cell_stats(ORDER[6] // 2, 0, EARLY + 1)
+            cell = EARLY + 1
+            for op in cell_sums(ORDER[6] // 2, 0, EARLY + 1) + last_sums(0, EARLY):
+                op()
+                if cell < 16:
+                    cell_stats(ORDER[6] // 2, cell, cell + 1)
+                    cell += 1
+            quantise_w(0)
             interleave_w(4)
-            token_scale(0, EARLY)
 
         with ExitStack() as pb:
-            npool = pb.enter_context(tc.tile_pool(name="npool", bufs=4))
             zpool = pb.enter_context(tc.tile_pool(name="zpool", bufs=3))
             cpool = pb.enter_context(tc.tile_pool(name="cpool", bufs=2))
             iopool = pb.enter_context(tc.tile_pool(name="iopool", bufs=2))
+            npool = pb.enter_context(tc.tile_pool(name="npool", bufs=4))
             pst = pb.enter_context(tc.psum_pool(name="pst", bufs=6))
             psm = pb.enter_context(tc.psum_pool(name="psm", bufs=2))
             pb.enter_context(tc.manual_schedule())
@@ -387,9 +406,11 @@ def tile_shiftedpatchtokenization_pb_t_kernel(tc, x, ln2_g, ln2_b, w2, b2, tok, 
 
             load(0)
             load(1)
-            for slot in range(10):
-                norm(0, slot)
-            add_bias(0)
+            for s in range(5):
+                norm(0, s)
+                norm(0, 5 + s)
+            late = cell_sums(ORDER[6] // 2, EARLY + 1, 16) + last_sums(EARLY, 16)
+            late = [late[0:2], late[2:4], late[4:6], late[6:8], late[8:9], late[9:10], [], late[10:11], [], late[11:13]]
             for r in range(16):
                 if r + 2 < 16:
                     load(r + 2)
@@ -423,25 +444,20 @@ def tile_shiftedpatchtokenization_pb_t_kernel(tc, x, ln2_g, ln2_b, w2, b2, tok, 
                         quantise_w(g5)
                     if g5 >= 1:
                         quantise(r, g5 - 1)
-                    if r == 0 and g5 < 4:
-                        cell_stats(ORDER[6] // 2, EARLY + 1 + 3 * g5, EARLY + 4 + 3 * g5)
-                    if r == 0 and g5 == 4:
-                        cell_sums(ORDER[6] // 2, EARLY + 1, 16)
-                    if r == 1 and g5 == 0:
-                        token_stats(EARLY, 16)
-                    if r == 1 and g5 == 2:
-                        token_root(EARLY, 16)
-                    if r == 1 and g5 == 3:
-                        token_scale(EARLY, 16)
-                    if r == 15 and g5 == 0:
+                    if r == 0 and g5 == 2:
+                        add_bias(0)
+                    for op in late[5 * r + g5 : 5 * r + g5 + 1]:
+                        for step in op:
+                            step()
+                    if r == 15 and g5 == 2:
                         project(14)
-                    if r == 15 and g5 >= 2:
-                        multiply(15, g5 - 2)
+                    if r == 15 and g5 >= 3:
+                        multiply(15, g5 - 3)
                 quantise(r, 4)
                 if 1 <= r < 15:
                     project(r - 1)
                 if r + 1 < 16:
                     add_bias(r + 1)
-            multiply(15, 3)
-            multiply(15, 4)
+            for g5 in range(2, 5):
+                multiply(15, g5)
             finish(15)

@@ -17,12 +17,15 @@ KDIM = 2560
 DIM = 512
 FLOPS = 2 * 4096 * KDIM * DIM
 
+ORDER = (6, 7, 0, 1, 2, 3, 4, 5)
+VECTOR_TAPS = (6,)
+EARLY = 3
+GROUPS = ((0, 2), (2, 4), (4, 5))
 ROW0 = (4, 0, 0, 8, 8)
 COL0 = (4, 0, 8, 0, 8)
-S_SLOTS = (1, 5, 7, 9)
-ORDER = (6, 7, 0, 1, 2, 3, 4, 5)
-VECTOR_TAPS = (3, 6, 9, 12)
-EARLY = 3
+SCALAR_NORMS = ((0, 1), (0, 4), (1, 3), (1, 4))
+BEFORE = (((0, 1), (0, 0), (1, 0)), ((0, 4), (0, 3), (1, 2)), ())
+AFTER = (((1, 1), (0, 2)), ((1, 3), (1, 4)), ())
 
 
 def tile_shiftedpatchtokenization_pb_t_kernel(tc, x, ln2_g, ln2_b, w2, b2, tok, out):
@@ -85,8 +88,23 @@ def tile_shiftedpatchtokenization_pb_t_kernel(tc, x, ln2_g, ln2_b, w2, b2, tok, 
         wraws = {}
         wgrps = {}
 
+        iopool = ctx.enter_context(tc.tile_pool(name="iopool", bufs=2))
+        tbs = {}
+        tks = {}
+
+        def load(r):
+            tks[r] = iopool.tile([P, 2, DIM], BF16, name="tk")
+            nc.sync.dma_start(out=tks[r][:], in_=tok_v[:, :, r, :])
+
+        def add_bias(r):
+            tb = iopool.tile([P, 2, DIM], F32, name="tb", bufs=3)
+            nc.vector.tensor_tensor(
+                out=tb[:], in0=tks[r][:], in1=b2bc[:].unsqueeze(1).to_broadcast([P, 2, DIM]), op=ALU.add
+            )
+            tbs[r] = tb
+
         def interleave_w(g5):
-            wgrps[g5] = wpool.tile([P, DIM, 4], BF16, name="wgrp", align_bytes=64, bufs=4)
+            wgrps[g5] = wpool.tile([P, DIM, 4], BF16, name="wgrp", align_bytes=64, bufs=3)
             raw = wraws[g5 // 2][:, 2 * (g5 % 2) : 2 * (g5 % 2) + 2, :]
             nc.scalar.copy(out=wgrps[g5][:], in_=raw.rearrange("p a (b n) -> p n (a b)", n=DIM))
 
@@ -157,7 +175,7 @@ def tile_shiftedpatchtokenization_pb_t_kernel(tc, x, ln2_g, ln2_b, w2, b2, tok, 
             ]
 
         with ExitStack() as pa:
-            xpool = pa.enter_context(tc.tile_pool(name="xpool", bufs=7))
+            xpool = pa.enter_context(tc.tile_pool(name="xpool", bufs=5))
             hpool = pa.enter_context(tc.tile_pool(name="hpool", bufs=4))
             tpool = pa.enter_context(tc.tile_pool(name="tpool", bufs=1))
             psa = pa.enter_context(tc.psum_pool(name="psa", bufs=4))
@@ -170,6 +188,10 @@ def tile_shiftedpatchtokenization_pb_t_kernel(tc, x, ln2_g, ln2_b, w2, b2, tok, 
             g0b = tpool.tile([P, P], BF16)
             g0f = tpool.tile([P, P], F32)
             nc.vector.memset(g0b[:], 0.0)
+            b2row = tpool.tile([P, DIM], BF16)
+            ones = tpool.tile([P, P], BF16)
+            nc.vector.memset(b2row[:], 0.0)
+            nc.vector.memset(ones[:], 1.0)
 
             pa.enter_context(tc.manual_schedule())
             xss = {}
@@ -202,12 +224,6 @@ def tile_shiftedpatchtokenization_pb_t_kernel(tc, x, ln2_g, ln2_b, w2, b2, tok, 
                 if k in VECTOR_TAPS:
                     nc.vector.tensor_tensor(out=hs[k][:], in0=hs[k][:], in1=xq[:, :, :, 1, :, 0], op=ALU.subtract)
 
-            def empty(n, i, out, in_):
-                if i == 7 and n % 2 == 1:
-                    nc.vector.tensor_copy(out=out, in_=in_)
-                else:
-                    nc.scalar.copy(out=out, in_=in_)
-
             def turn_first(k):
                 i, hq = divmod(k, 2)
                 h = hs[k]
@@ -230,9 +246,9 @@ def tile_shiftedpatchtokenization_pb_t_kernel(tc, x, ln2_g, ln2_b, w2, b2, tok, 
                                 out=p1s[o][:, gq, :], lhsT=xq[:, gq, o, 1, :, tap], rhs=neg_id[:],
                                 start=False, stop=(tap == 1 and gq == 3),
                             )
-                    empty(
-                        o, i, m_v[:, :, o, :, 4 * hq : 4 * hq + 4],
-                        p1s[o][:].rearrange("p q (b c) -> p c b q", c=8),
+                    nc.scalar.copy(
+                        out=m_v[:, :, o, :, 4 * hq : 4 * hq + 4],
+                        in_=p1s[o][:].rearrange("p q (b c) -> p c b q", c=8),
                     )
 
             def turn_second(k):
@@ -253,16 +269,13 @@ def tile_shiftedpatchtokenization_pb_t_kernel(tc, x, ln2_g, ln2_b, w2, b2, tok, 
                         dst = W[:, r, 4:132, 4 * ch : 4 * ch + 4]
                         srcv = p2[:].rearrange("p c x -> p x c")
                         if mask is None:
-                            empty(ch, i, dst, srcv)
-                        elif ch == 0:
-                            nc.scalar.activation(out=dst, in_=srcv, func=ACT.Copy, scale=mask[:, 0:1])
+                            nc.scalar.copy(out=dst, in_=srcv)
                         else:
-                            nc.vector.tensor_scalar(
-                                out=dst, in0=srcv, scalar1=mask[:, 0:1], scalar2=None, op0=ALU.mult
-                            )
+                            nc.scalar.activation(out=dst, in_=srcv, func=ACT.Copy, scale=mask[:, 0:1])
 
             load_half(0)
             load_half(1)
+            nc.sync.dma_start(out=b2row[0:1, :], in_=b2.unsqueeze(0))
             load_half(2)
             load_half(3)
             for row0, vec in ((0, ln2_g), (32, ln2_b)):
@@ -271,9 +284,8 @@ def tile_shiftedpatchtokenization_pb_t_kernel(tc, x, ln2_g, ln2_b, w2, b2, tok, 
                     in_=vec.rearrange("(y j q) -> j y q", y=16, q=8),
                 )
             load_half(4)
-            load_half(5)
-            load_half(6)
-            nc.sync.dma_start(out=b2bc[:], in_=b2.partition_broadcast(P))
+            load(0)
+            load(1)
 
             for k in range(20):
                 if k >= 8:
@@ -283,16 +295,35 @@ def tile_shiftedpatchtokenization_pb_t_kernel(tc, x, ln2_g, ln2_b, w2, b2, tok, 
                     if part == 3:
                         for op in cell_sums(q, 0, 16):
                             op()
+                if k == 16:
+                    moved = psa.tile([P, 2, 2, 32], F32, name="p1")
+                    for n, shifter, cell_row in ((0, sh_dn, 4), (1, sh_up, 1)):
+                        nc.tensor.matmul(
+                            out=moved[:, n], lhsT=shifter[:], rhs=CR[:, :, cell_row, 1:33], start=True, stop=True
+                        )
+                if k == 18:
+                    nc.vector.tensor_copy(out=CR[:, :, 0, 1:33], in_=moved[:, 0])
+                    nc.vector.tensor_copy(out=CR[:, :, 5, 1:33], in_=moved[:, 1])
                 if k == 19:
                     first_sums()
                 if k < 16:
                     haar(k)
                 if k >= 2 and k - 2 < 16:
                     turn_first(k - 2)
-                if 2 <= k <= 10:
-                    load_half(k + 5)
-                if 11 <= k <= 13:
-                    load_w(k - 11)
+                if 2 <= k <= 12:
+                    load_half(k + 3)
+                if 13 <= k <= 15:
+                    load_w(k - 13)
+                if k == 4:
+                    b2ps = psa.tile([P, 4, P], F32, name="p2")
+                    nc.tensor.matmul(
+                        out=b2ps[:].rearrange("p a b -> p (a b)"), lhsT=ones[:], rhs=b2row[:], start=True, stop=True
+                    )
+                    nc.scalar.copy(out=b2bc[:], in_=b2ps[:].rearrange("p a b -> p (a b)"))
+                if 5 <= k <= 7:
+                    add_bias(k - 5)
+                if k == 5:
+                    load(2)
                 if k == 4:
                     nc.vector.tensor_copy(out=g0f[:], in_=g0b[:])
                 if k >= 4:
@@ -301,16 +332,9 @@ def tile_shiftedpatchtokenization_pb_t_kernel(tc, x, ln2_g, ln2_b, w2, b2, tok, 
                     gps = psa.tile([P, 4, P], F32, name="p2")
                     nc.tensor.transpose(gps[:, 0, :], g0f[:], ident[:])
                     nc.scalar.copy(out=gb[:], in_=gps[:, 0, :])
-                if k == 17:
-                    moved = psa.tile([P, 2, 2, 32], F32, name="p1")
-                    for n, shifter, cell_row in ((0, sh_dn, 4), (1, sh_up, 1)):
-                        nc.tensor.matmul(
-                            out=moved[:, n], lhsT=shifter[:], rhs=CR[:, :, cell_row, 1:33], start=True, stop=True
-                        )
-                    nc.vector.tensor_copy(out=CR[:, :, 0, 1:33], in_=moved[:, 0])
-                    nc.vector.tensor_copy(out=CR[:, :, 5, 1:33], in_=moved[:, 1])
-            for g5 in range(4):
+            for g5 in range(3):
                 interleave_w(g5)
+            quantise_w(0)
             cell_stats(ORDER[6] // 2, 0, EARLY + 1)
             cell = EARLY + 1
             for op in cell_sums(ORDER[6] // 2, 0, EARLY + 1) + last_sums(0, EARLY):
@@ -318,146 +342,132 @@ def tile_shiftedpatchtokenization_pb_t_kernel(tc, x, ln2_g, ln2_b, w2, b2, tok, 
                 if cell < 16:
                     cell_stats(ORDER[6] // 2, cell, cell + 1)
                     cell += 1
-            quantise_w(0)
+                if cell == 10:
+                    quantise_w(1)
+            interleave_w(3)
             interleave_w(4)
 
         with ExitStack() as pb:
             zpool = pb.enter_context(tc.tile_pool(name="zpool", bufs=3))
-            cpool = pb.enter_context(tc.tile_pool(name="cpool", bufs=2))
-            iopool = pb.enter_context(tc.tile_pool(name="iopool", bufs=2))
+            cpool = pb.enter_context(tc.tile_pool(name="cpool", bufs=3))
             npool = pb.enter_context(tc.tile_pool(name="npool", bufs=4))
             pst = pb.enter_context(tc.psum_pool(name="pst", bufs=6))
             psm = pb.enter_context(tc.psum_pool(name="psm", bufs=2))
             pb.enter_context(tc.manual_schedule())
 
             nbs = {}
-            tbs = {}
-            tks = {}
             codes = {}
+            zps = {}
             zis = {}
             accs = {}
 
-            def load(r):
-                tks[r] = iopool.tile([P, 2, DIM], BF16, name="tk", bufs=3)
-                nc.sync.dma_start(out=tks[r][:], in_=tok_v[:, :, r, :])
-
-            def add_bias(r):
-                tb = iopool.tile([P, 2, DIM], F32, name="tb", bufs=3)
-                nc.vector.tensor_tensor(
-                    out=tb[:], in0=tks[r][:], in1=b2bc[:].unsqueeze(1).to_broadcast([P, 2, DIM]), op=ALU.add
-                )
-                tbs[r] = tb
-
-            def norm(r, slot):
-                e, s = divmod(slot, 5)
-                if s == 0:
+            def norm(r, e, s):
+                if (r, e) not in nbs:
                     nbs[(r, e)] = npool.tile([P, KDIM], F32, name="nb")
-                nbv = nbs[(r, e)][:].rearrange("p (z s a h c) -> p s a h z c", z=4, s=5, a=8, h=2)
-                srcw = W[:, 8 * e + ROW0[s] : 8 * e + ROW0[s] + 8, 8 * r + COL0[s] : 8 * r + COL0[s] + 8, :].rearrange("p a (h z) c -> p a h z c", z=4)
-                if slot in S_SLOTS and r > 0:
-                    nc.scalar.activation(
-                        out=nbv[:, s], in_=srcw, func=ACT.Identity,
-                        scale=rstd[:, e, r : r + 1], bias=nbias[:, e, r : r + 1],
-                    )
+                dst = nbs[(r, e)][:].rearrange("p (z s a h c) -> p s a h z c", z=4, s=5, a=8, h=2)[:, s]
+                row, col = 8 * e + ROW0[s], 8 * r + COL0[s]
+                src = W[:, row : row + 8, col : col + 8, :].rearrange("p a (h z) c -> p a h z c", z=4)
+                scale, bias = rstd[:, e, r : r + 1], nbias[:, e, r : r + 1]
+                if (e, s) in SCALAR_NORMS and r > 0:
+                    nc.scalar.activation(out=dst, in_=src, func=ACT.Identity, scale=scale, bias=bias)
                 else:
                     nc.vector.tensor_scalar(
-                        out=nbv[:, s], in0=srcw,
-                        scalar1=rstd[:, e, r : r + 1], scalar2=nbias[:, e, r : r + 1],
-                        op0=ALU.mult, op1=ALU.add,
+                        out=dst, in0=src, scalar1=scale, scalar2=bias, op0=ALU.mult, op1=ALU.add
                     )
 
-            def quantise(r, g5):
-                zc, zs = codes[r]
-                nc.vector.quantize_mx(
-                    out=zc[:, g5, :].bitcast(FP8X4), scales=zs[:, g5, :],
-                    in_=zis[(r, g5)][:].rearrange("p c t -> p (c t)"),
+            def turn(r, g5, zp):
+                for half in range(2):
+                    pt = pst.tile([P, 2, 2, P], F32, name="pt")
+                    for a in range(2):
+                        sl = 4 * g5 + 2 * half + a
+                        for u in range(2):
+                            nc.tensor.transpose(pt[:, a, u, :], nbs[(r, u)][:, P * sl : P * sl + P], ident[:])
+                    for a in range(2):
+                        sl = 4 * g5 + 2 * half + a
+                        nc.scalar.activation(
+                            out=zp[:, 2 * half + a, :], in_=pt[:, a, :, :].rearrange("p u r -> p (u r)"),
+                            func=ACT.Identity, scale=gb[:, sl : sl + 1], bias=gb[:, 32 + sl : 33 + sl],
+                        )
+
+            def interleave(r, first, last):
+                n = last - first
+                zi = zpool.tile([P, 2, 256, 4], BF16, name="zi", align_bytes=64)
+                zis[(r, first)] = zi
+                nc.vector.tensor_copy(
+                    out=zi[:, 0:n].rearrange("p g (c i) t -> p (g c) t i", i=4),
+                    in_=zps[(r, first)][:, :, 0:n].rearrange("p t g (c i) -> p (g c) t i", i=4),
                 )
 
-            def multiply(r, g5, us=(0, 1)):
+            def quantise(r, first, last):
+                n = last - first
                 zc, zs = codes[r]
-                for u in us:
-                    if g5 == 0:
-                        acc = psm.tile([P, DIM], F32, name="acc")
-                        accs[(r, u)] = acc
-                    nc.tensor.matmul_mx(
-                        out=accs[(r, u)][:],
-                        lhsT=zc[:, g5, P * u : P * u + P].bitcast(FP8X4),
-                        lhsT_scale=zs[:, g5, P * u : P * u + P],
-                        rhs=wc[:, g5, :].bitcast(FP8X4),
-                        rhs_scale=ws[:, g5, :],
-                        start=(g5 == 0),
-                        stop=(g5 == 4),
-                    )
+                nc.vector.quantize_mx(
+                    out=zc[:, first:last, :].rearrange("p g c -> p (g c)").bitcast(FP8X4),
+                    scales=zs[:, first:last, :].rearrange("p g c -> p (g c)"),
+                    in_=zis[(r, first)][:, 0:n].rearrange("p g c t -> p (g c t)"),
+                )
 
-            def finish(r):
-                tb = tbs[r]
+            def multiply(r):
+                zc, zs = codes[r]
                 for u in range(2):
-                    nc.vector.tensor_tensor(out=tb[:, u, :], in0=accs[(r, u)][:], in1=tb[:, u, :], op=ALU.add)
-                    if r == 15:
-                        nc.sync.dma_start(out=out_v[:, u, r, :], in_=tb[:, u, :])
-                if r < 15:
+                    acc = psm.tile([P, DIM], F32, name="acc")
+                    accs[(r, u)] = acc
+                    for g5 in range(5):
+                        nc.tensor.matmul_mx(
+                            out=acc[:],
+                            lhsT=zc[:, g5, P * u : P * u + P].bitcast(FP8X4),
+                            lhsT_scale=zs[:, g5, P * u : P * u + P],
+                            rhs=wc[:, g5, :].bitcast(FP8X4),
+                            rhs_scale=ws[:, g5, :],
+                            start=(g5 == 0),
+                            stop=(g5 == 4),
+                        )
+
+            def add_up(r, u):
+                tb = tbs[r]
+                nc.vector.tensor_tensor(out=tb[:, u, :], in0=accs[(r, u)][:], in1=tb[:, u, :], op=ALU.add)
+                if r == 15:
+                    nc.sync.dma_start(out=out_v[:, u, r, :], in_=tb[:, u, :])
+                elif u == 1:
                     nc.sync.dma_start(out=out_v[:, :, r, :], in_=tb[:])
 
-            def project(r):
-                for u in range(2):
-                    for g5 in range(5):
-                        multiply(r, g5, (u,))
-                finish(r)
-
-            load(0)
-            load(1)
             for s in range(5):
-                norm(0, s)
-                norm(0, 5 + s)
+                norm(0, 0, s)
+                norm(0, 1, s)
             late = cell_sums(ORDER[6] // 2, EARLY + 1, 16) + last_sums(EARLY, 16)
-            late = [late[0:2], late[2:4], late[4:6], late[6:8], late[8:9], late[9:10], [], late[10:11], [], late[11:13]]
+            late = [late[0:3], late[3:6], late[6:8], late[8:10], late[10:11], late[11:13]]
             for r in range(16):
-                if r + 2 < 16:
-                    load(r + 2)
+                if 2 <= r < 15:
+                    load(r + 1)
                 zc_t = cpool.tile([P, 5, 256], U32, name="zc", align_bytes=64)
                 zs_t = cpool.tile([P, 5, 256], U8, name="zs", align_bytes=64)
                 codes[r] = (zc_t, zs_t)
-                for g5 in range(5):
-                    zp = zpool.tile([P, 4, 256], BF16, name="zp")
-                    for half in range(2):
-                        pt = pst.tile([P, 2, 2, P], F32, name="pt")
-                        for a in range(2):
-                            sl = 4 * g5 + 2 * half + a
-                            for u in range(2):
-                                nc.tensor.transpose(pt[:, a, u, :], nbs[(r, u)][:, P * sl : P * sl + P], ident[:])
-                        for a in range(2):
-                            sl = 4 * g5 + 2 * half + a
-                            nc.scalar.activation(
-                                out=zp[:, 2 * half + a, :], in_=pt[:, a, :, :].rearrange("p u r -> p (u r)"),
-                                func=ACT.Identity, scale=gb[:, sl : sl + 1], bias=gb[:, 32 + sl : 33 + sl],
-                            )
-                    if r + 1 < 16:
-                        norm(r + 1, 2 * g5)
-                        norm(r + 1, 2 * g5 + 1)
-                    zi = zpool.tile([P, 256, 4], BF16, name="zi", align_bytes=64)
-                    zis[(r, g5)] = zi
-                    nc.vector.tensor_copy(
-                        out=zi[:].rearrange("p (c i) t -> p c t i", i=4),
-                        in_=zp[:].rearrange("p t (c i) -> p c t i", i=4),
-                    )
-                    if r == 0 and g5 >= 1:
-                        quantise_w(g5)
-                    if g5 >= 1:
-                        quantise(r, g5 - 1)
-                    if r == 0 and g5 == 2:
-                        add_bias(0)
-                    for op in late[5 * r + g5 : 5 * r + g5 + 1]:
-                        for step in op:
+                for n, (first, last) in enumerate(GROUPS):
+                    zp = zpool.tile([P, 4, 2, 256], BF16, name="zp")
+                    zps[(r, first)] = zp
+                    for g5 in range(first, last):
+                        turn(r, g5, zp[:, :, g5 - first])
+                    if n == 1 and r >= 1:
+                        multiply(r - 1)
+                    if n == 2 and r >= 1:
+                        add_up(r - 1, 0)
+                    if r < 15:
+                        for e, part in BEFORE[n]:
+                            norm(r + 1, e, part)
+                    interleave(r, first, last)
+                    if r < 15:
+                        for e, part in AFTER[n]:
+                            norm(r + 1, e, part)
+                    if n == 2 and r >= 1:
+                        add_up(r - 1, 1)
+                    if r == 0:
+                        quantise_w(2 + n)
+                    quantise(r, first, last)
+                    if r < 2:
+                        for step in late[3 * r + n]:
                             step()
-                    if r == 15 and g5 == 2:
-                        project(14)
-                    if r == 15 and g5 >= 3:
-                        multiply(15, g5 - 3)
-                quantise(r, 4)
-                if 1 <= r < 15:
-                    project(r - 1)
-                if r + 1 < 16:
+                if 2 <= r < 15:
                     add_bias(r + 1)
-            for g5 in range(2, 5):
-                multiply(15, g5)
-            finish(15)
+            multiply(15)
+            add_up(15, 0)
+            add_up(15, 1)

from contextlib import ExitStack

import concourse.mybir as mybir
from concourse.masks import make_identity

F32 = mybir.dt.float32
BF16 = mybir.dt.bfloat16
U32 = mybir.dt.uint32
U8 = mybir.dt.uint8
FP8X4 = mybir.dt.float8_e4m3fn_x4
ALU = mybir.AluOpType
ACT = mybir.ActivationFunctionType
AX = mybir.AxisListType

P = 128
KDIM = 2560
DIM = 512
FLOPS = 2 * 4096 * KDIM * DIM

ORDER = (6, 7, 0, 1, 2, 3, 4, 5)
VECTOR_TAPS = (6,)
EARLY = 3
GROUPS = ((0, 2), (2, 4), (4, 5))
ROW0 = (4, 0, 0, 8, 8)
COL0 = (4, 0, 8, 0, 8)
SCALAR_NORMS = ((0, 1), (0, 4), (1, 3), (1, 4))
BEFORE = (((0, 1), (0, 0), (1, 0)), ((0, 4), (0, 3), (1, 2)), ())
AFTER = (((1, 1), (0, 2)), ((1, 3), (1, 4)), ())


def tile_shiftedpatchtokenization_pb_t_kernel(tc, x, ln2_g, ln2_b, w2, b2, tok, out):
    nc = tc.nc
    xv = x.rearrange("b c (g u r) w -> (b c) g u (r w)", g=8, u=8)
    wv = w2.rearrange("(y j q) n -> q y j n", y=16, q=8)
    tok_v = tok.rearrange("b (g e j) d -> (b g) e j d", g=8, e=2)
    out_v = out.rearrange("b (g e j) d -> (b g) e j d", g=8, e=2)

    with ExitStack() as ctx:
        keep = ctx.enter_context(tc.tile_pool(name="keep", bufs=1))
        ident = keep.tile([P, P], F32)
        sh_dn = keep.tile([P, P], F32)
        sh_up = keep.tile([P, P], F32)
        gb = keep.tile([P, P], F32)
        b2bc = keep.tile([P, DIM], BF16)
        wc = keep.tile([P, 5, DIM], U32, align_bytes=64)
        ws = keep.tile([P, 5, DIM], U8, align_bytes=64)
        W = keep.tile([P, 24, 136, 8], F32)
        bns = keep.tile([P, 4, 16, 6], F32)
        sq_a = keep.tile([P, 32], F32)
        CR = keep.tile([P, 2, 6, 34], F32)
        A1 = keep.tile([P, 2, 5, 34], F32)
        Rw = keep.tile([P, 2, 2, 34], F32)
        Bw = keep.tile([P, 2, 2, 33], F32)
        Bc = keep.tile([P, 2, 2, 33], F32)
        ST = keep.tile([P, 2, 2, 16], F32)
        D3 = keep.tile([P, 2, 33], F32)
        F3 = keep.tile([P, 2, 16], F32)
        G3 = keep.tile([P, 2, 16], F32)
        tmp = keep.tile([P, 2, 16], F32)
        rstd = keep.tile([P, 2, 16], F32)
        nbias = keep.tile([P, 2, 16], F32)
        one = keep.tile([P, 1], F32)
        mask_top = keep.tile([P, 1], F32)
        mask_bot = keep.tile([P, 1], F32)
        neg_id = keep.tile([P, P], BF16)

        nc.vector.memset(one[:], 1.0)
        nc.scalar.sqrt(one[:], one[:])

        make_identity(nc, ident[:])
        id8 = ident[:].rearrange("p (a b) -> p a b", b=8)
        nc.vector.tensor_scalar(out=neg_id[:], in0=ident[:], scalar1=-1.0, scalar2=None, op0=ALU.mult)
        nc.vector.memset(sh_dn[:], 0.0)
        nc.vector.memset(sh_up[:], 0.0)
        nc.vector.tensor_copy(out=sh_dn[:, 1:P], in_=ident[:, 0 : P - 1])
        nc.vector.tensor_copy(out=sh_up[:, 0 : P - 1], in_=ident[:, 1:P])
        nc.vector.memset(sh_dn[:].rearrange("p (a b) -> p a b", b=8)[:, :, 0:1], 0.0)
        nc.vector.memset(sh_up[:].rearrange("p (a b) -> p a b", b=8)[:, :, 7:8], 0.0)
        nc.vector.tensor_reduce(out=mask_top[:], in_=id8[:, :, 0], axis=AX.X, op=ALU.add)
        nc.vector.tensor_reduce(out=mask_bot[:], in_=id8[:, :, 7], axis=AX.X, op=ALU.add)
        nc.vector.tensor_scalar(out=mask_top[:], in0=mask_top[:], scalar1=-1.0, scalar2=1.0, op0=ALU.mult, op1=ALU.add)
        nc.vector.tensor_scalar(out=mask_bot[:], in0=mask_bot[:], scalar1=-1.0, scalar2=1.0, op0=ALU.mult, op1=ALU.add)
        nc.vector.memset(W[:, :, 0:4, :], 0.0)
        nc.vector.memset(W[:, :, 132:136, :], 0.0)
        nc.vector.memset(CR[:], 0.0)

        wpool = ctx.enter_context(tc.tile_pool(name="wpool", bufs=1))
        wraws = {}
        wgrps = {}

        iopool = ctx.enter_context(tc.tile_pool(name="iopool", bufs=2))
        tbs = {}
        tks = {}

        def load(r):
            tks[r] = iopool.tile([P, 2, DIM], BF16, name="tk")
            nc.sync.dma_start(out=tks[r][:], in_=tok_v[:, :, r, :])

        def add_bias(r):
            tb = iopool.tile([P, 2, DIM], F32, name="tb", bufs=3)
            nc.vector.tensor_tensor(
                out=tb[:], in0=tks[r][:], in1=b2bc[:].unsqueeze(1).to_broadcast([P, 2, DIM]), op=ALU.add
            )
            tbs[r] = tb

        def interleave_w(g5):
            wgrps[g5] = wpool.tile([P, DIM, 4], BF16, name="wgrp", align_bytes=64, bufs=3)
            raw = wraws[g5 // 2][:, 2 * (g5 % 2) : 2 * (g5 % 2) + 2, :]
            nc.scalar.copy(out=wgrps[g5][:], in_=raw.rearrange("p a (b n) -> p n (a b)", n=DIM))

        def quantise_w(g5):
            nc.vector.quantize_mx(
                out=wc[:, g5, :].bitcast(FP8X4),
                scales=ws[:, g5, :],
                in_=wgrps[g5][:].rearrange("p n t -> p (n t)"),
            )

        def cell_stats(q, first, last):
            r0 = 4 + 4 * q
            for cx in range(first, last):
                nc.vector.bn_stats(
                    out=bns[:, q, cx, :],
                    in_=W[:, r0 : r0 + 4, 4 + 8 * cx : 12 + 8 * cx, :].rearrange("p y (v x) c -> p y (x c) v", v=2),
                )

        def cell_sums(q, first, last):
            cells = bns[:, q, first:last, :].rearrange("p a (v f) -> p (a v) f", v=2)
            sums = CR[:, :, 1 + q, 1 + 2 * first : 1 + 2 * last]
            sq = sq_a[:, 2 * first : 2 * last]
            return [
                lambda: nc.vector.scalar_tensor_tensor(
                    out=sq, in0=cells[:, :, 1], scalar=128.0 / KDIM, in1=cells[:, :, 1], op0=ALU.mult, op1=ALU.mult
                ),
                lambda: nc.vector.tensor_copy(out=sums[:, 0], in_=cells[:, :, 1]),
                lambda: nc.vector.scalar_tensor_tensor(
                    out=sums[:, 1], in0=cells[:, :, 2], scalar=1.0 / KDIM, in1=sq, op0=ALU.mult, op1=ALU.add
                ),
            ]

        def first_sums():
            nc.vector.tensor_tensor(out=A1[:], in0=CR[:, :, 0:5, :], in1=CR[:, :, 1:6, :], op=ALU.add)
            nc.vector.tensor_tensor(out=Rw[:], in0=A1[:, :, 0:3:2, :], in1=A1[:, :, 2:5:2, :], op=ALU.add)
            nc.vector.tensor_tensor(out=Bc[:], in0=A1[:, :, 1:4:2, 0:33], in1=A1[:, :, 1:4:2, 1:34], op=ALU.add)
            nc.vector.tensor_tensor(out=Bw[:], in0=Rw[:, :, :, 0:33], in1=Rw[:, :, :, 1:34], op=ALU.add)
            nc.vector.tensor_tensor(out=ST[:], in0=Bw[:, :, :, 0:31:2], in1=Bw[:, :, :, 2:33:2], op=ALU.add)
            nc.vector.tensor_tensor(out=ST[:], in0=ST[:], in1=Bc[:, :, :, 1:32:2], op=ALU.add)
            nc.vector.tensor_scalar(out=ST[:, 1], in0=ST[:, 1], scalar1=36.0e-5, scalar2=None, op0=ALU.add)

        def last_sums(j0, j1):
            a, b = 2 * j0, 2 * j1 + 2
            row, pair, four, six = CR[:, :, 3, :], D3[:, :, a : b - 1], F3[:, :, j0:j1], G3[:, :, j0:j1]
            st = ST[:, :, :, j0:j1]
            t, r, n = (z[:, :, j0:j1] for z in (tmp, rstd, nbias))
            c = 128.0 / KDIM

            def add(out, in0, in1):
                return lambda: nc.vector.tensor_tensor(out=out, in0=in0, in1=in1, op=ALU.add)

            def product(out, in0, scalar, in1):
                return lambda: nc.vector.scalar_tensor_tensor(
                    out=out, in0=in0, scalar=scalar, in1=in1, op0=ALU.mult, op1=ALU.mult
                )

            return [
                add(pair, row[:, :, a : b - 1], row[:, :, a + 1 : b]),
                add(four, D3[:, :, a : b - 3 : 2], D3[:, :, a + 2 : b - 1 : 2]),
                add(six, four, D3[:, :, a + 1 : b - 2 : 2]),
                add(st[:, :, 0], st[:, :, 0], four),
                add(st[:, :, 1], st[:, :, 1], six),
                product(t, st[:, 0], -c * c, st[:, 0]),
                add(t, t, st[:, 1]),
                lambda: nc.scalar.sqrt(t, t),
                lambda: nc.vector.reciprocal(r, t),
                product(n, st[:, 0], -c, r),
            ]

        with ExitStack() as pa:
            xpool = pa.enter_context(tc.tile_pool(name="xpool", bufs=5))
            hpool = pa.enter_context(tc.tile_pool(name="hpool", bufs=4))
            tpool = pa.enter_context(tc.tile_pool(name="tpool", bufs=1))
            psa = pa.enter_context(tc.psum_pool(name="psa", bufs=4))

            m_a = tpool.tile([P, 2056], F32)
            m_b = tpool.tile([P, 2056], F32)
            for m_t in (m_a, m_b):
                nc.vector.memset(m_t[:, 0:4], 0.0)
                nc.vector.memset(m_t[:, 2052:2056], 0.0)
            g0b = tpool.tile([P, P], BF16)
            g0f = tpool.tile([P, P], F32)
            nc.vector.memset(g0b[:], 0.0)
            b2row = tpool.tile([P, DIM], BF16)
            ones = tpool.tile([P, P], BF16)
            nc.vector.memset(b2row[:], 0.0)
            nc.vector.memset(ones[:], 1.0)

            pa.enter_context(tc.manual_schedule())
            xss = {}
            hs = {}

            def load_half(k):
                i, hq = divmod(k, 2)
                xss[k] = xpool.tile([P, 4, 1024], BF16, name="xs")
                nc.sync.dma_start(out=xss[k][:], in_=xv[:, 4 * hq : 4 * hq + 4, ORDER[i], :])

            def load_w(m):
                wraws[m] = xpool.tile([P, 4, 1024], BF16, name="xs")
                slots = min(8, 20 - 8 * m)
                for q in range(8):
                    nc.sync.dma_start(
                        out=wraws[m][q:P:8, 0 : slots // 2, :].rearrange("y a (b n) -> y (a b) n", n=DIM),
                        in_=wv[q, :, 8 * m : 8 * m + slots, :],
                    )

            def taps(k):
                return xss[k][:].rearrange("p g (o e x f) -> p g o e x f", o=2, e=2, x=128, f=2)

            def haar(k):
                xq = taps(k)
                hs[k] = hpool.tile([P, 4, 2, 128], F32, name="h")
                nc.vector.scalar_tensor_tensor(
                    out=hs[k][:], in0=xq[:, :, :, 0, :, 0], scalar=3.0, in1=xq[:, :, :, 0, :, 1],
                    op0=ALU.mult, op1=ALU.subtract,
                )
                if k in VECTOR_TAPS:
                    nc.vector.tensor_tensor(out=hs[k][:], in0=hs[k][:], in1=xq[:, :, :, 1, :, 0], op=ALU.subtract)

            def turn_first(k):
                i, hq = divmod(k, 2)
                h = hs[k]
                xq = taps(k)
                m_t = m_a if i % 2 == 0 else m_b
                m_v = m_t[:, 4:2052].rearrange("p (c o b g) -> p c o b g", c=8, o=2, b=16)
                p1s = []
                for o in range(2):
                    p1 = psa.tile([P, 4, P], F32, name="p1")
                    p1s.append(p1)
                    for gq in range(4):
                        nc.tensor.matmul(
                            out=p1[:, gq, :], lhsT=h[:, gq, o, :], rhs=ident[:],
                            is_transpose=True, start=(gq == 0), stop=False,
                        )
                for o in range(2):
                    for tap in (1,) if k in VECTOR_TAPS else (0, 1):
                        for gq in range(4):
                            nc.tensor.matmul(
                                out=p1s[o][:, gq, :], lhsT=xq[:, gq, o, 1, :, tap], rhs=neg_id[:],
                                start=False, stop=(tap == 1 and gq == 3),
                            )
                    nc.scalar.copy(
                        out=m_v[:, :, o, :, 4 * hq : 4 * hq + 4],
                        in_=p1s[o][:].rearrange("p q (b c) -> p c b q", c=8),
                    )

            def turn_second(k):
                i, o = divmod(k, 2)
                m_t = m_a if i % 2 == 0 else m_b
                ro = 2 * ORDER[i] + o
                jobs = [(4 + ro, 0, None)]
                if ro < 4:
                    jobs.append((20 + ro, 1, mask_bot))
                if ro >= 12:
                    jobs.append((ro - 12, -1, mask_top))
                for r, shift, mask in jobs:
                    for ch in range(2):
                        p2 = psa.tile([P, 4, P], F32, name="p2")
                        for c4 in range(4):
                            base = 4 + ((4 * ch + c4) * 2 + o) * P + shift
                            nc.tensor.transpose(p2[:, c4, :], m_t[:, base : base + P], ident[:])
                        dst = W[:, r, 4:132, 4 * ch : 4 * ch + 4]
                        srcv = p2[:].rearrange("p c x -> p x c")
                        if mask is None:
                            nc.scalar.copy(out=dst, in_=srcv)
                        else:
                            nc.scalar.activation(out=dst, in_=srcv, func=ACT.Copy, scale=mask[:, 0:1])

            load_half(0)
            load_half(1)
            nc.sync.dma_start(out=b2row[0:1, :], in_=b2.unsqueeze(0))
            load_half(2)
            load_half(3)
            for row0, vec in ((0, ln2_g), (32, ln2_b)):
                nc.sync.dma_start(
                    out=g0b[row0 : row0 + 20, :].rearrange("j (y q) -> j y q", q=8),
                    in_=vec.rearrange("(y j q) -> j y q", y=16, q=8),
                )
            load_half(4)
            load(0)
            load(1)

            for k in range(20):
                if k >= 8:
                    q, part = divmod(k - 8, 4)
                    q = ORDER[2 * q] // 2
                    cell_stats(q, 4 * part, 4 * part + 4)
                    if part == 3:
                        for op in cell_sums(q, 0, 16):
                            op()
                if k == 16:
                    moved = psa.tile([P, 2, 2, 32], F32, name="p1")
                    for n, shifter, cell_row in ((0, sh_dn, 4), (1, sh_up, 1)):
                        nc.tensor.matmul(
                            out=moved[:, n], lhsT=shifter[:], rhs=CR[:, :, cell_row, 1:33], start=True, stop=True
                        )
                if k == 18:
                    nc.vector.tensor_copy(out=CR[:, :, 0, 1:33], in_=moved[:, 0])
                    nc.vector.tensor_copy(out=CR[:, :, 5, 1:33], in_=moved[:, 1])
                if k == 19:
                    first_sums()
                if k < 16:
                    haar(k)
                if k >= 2 and k - 2 < 16:
                    turn_first(k - 2)
                if 2 <= k <= 12:
                    load_half(k + 3)
                if 13 <= k <= 15:
                    load_w(k - 13)
                if k == 4:
                    b2ps = psa.tile([P, 4, P], F32, name="p2")
                    nc.tensor.matmul(
                        out=b2ps[:].rearrange("p a b -> p (a b)"), lhsT=ones[:], rhs=b2row[:], start=True, stop=True
                    )
                    nc.scalar.copy(out=b2bc[:], in_=b2ps[:].rearrange("p a b -> p (a b)"))
                if 5 <= k <= 7:
                    add_bias(k - 5)
                if k == 5:
                    load(2)
                if k == 4:
                    nc.vector.tensor_copy(out=g0f[:], in_=g0b[:])
                if k >= 4:
                    turn_second(k - 4)
                if k == 7:
                    gps = psa.tile([P, 4, P], F32, name="p2")
                    nc.tensor.transpose(gps[:, 0, :], g0f[:], ident[:])
                    nc.scalar.copy(out=gb[:], in_=gps[:, 0, :])
            for g5 in range(3):
                interleave_w(g5)
            quantise_w(0)
            cell_stats(ORDER[6] // 2, 0, EARLY + 1)
            cell = EARLY + 1
            for op in cell_sums(ORDER[6] // 2, 0, EARLY + 1) + last_sums(0, EARLY):
                op()
                if cell < 16:
                    cell_stats(ORDER[6] // 2, cell, cell + 1)
                    cell += 1
                if cell == 10:
                    quantise_w(1)
            interleave_w(3)
            interleave_w(4)

        with ExitStack() as pb:
            zpool = pb.enter_context(tc.tile_pool(name="zpool", bufs=3))
            cpool = pb.enter_context(tc.tile_pool(name="cpool", bufs=3))
            npool = pb.enter_context(tc.tile_pool(name="npool", bufs=4))
            pst = pb.enter_context(tc.psum_pool(name="pst", bufs=6))
            psm = pb.enter_context(tc.psum_pool(name="psm", bufs=2))
            pb.enter_context(tc.manual_schedule())

            nbs = {}
            codes = {}
            zps = {}
            zis = {}
            accs = {}

            def norm(r, e, s):
                if (r, e) not in nbs:
                    nbs[(r, e)] = npool.tile([P, KDIM], F32, name="nb")
                dst = nbs[(r, e)][:].rearrange("p (z s a h c) -> p s a h z c", z=4, s=5, a=8, h=2)[:, s]
                row, col = 8 * e + ROW0[s], 8 * r + COL0[s]
                src = W[:, row : row + 8, col : col + 8, :].rearrange("p a (h z) c -> p a h z c", z=4)
                scale, bias = rstd[:, e, r : r + 1], nbias[:, e, r : r + 1]
                if (e, s) in SCALAR_NORMS and r > 0:
                    nc.scalar.activation(out=dst, in_=src, func=ACT.Identity, scale=scale, bias=bias)
                else:
                    nc.vector.tensor_scalar(
                        out=dst, in0=src, scalar1=scale, scalar2=bias, op0=ALU.mult, op1=ALU.add
                    )

            def turn(r, g5, zp):
                for half in range(2):
                    pt = pst.tile([P, 2, 2, P], F32, name="pt")
                    for a in range(2):
                        sl = 4 * g5 + 2 * half + a
                        for u in range(2):
                            nc.tensor.transpose(pt[:, a, u, :], nbs[(r, u)][:, P * sl : P * sl + P], ident[:])
                    for a in range(2):
                        sl = 4 * g5 + 2 * half + a
                        nc.scalar.activation(
                            out=zp[:, 2 * half + a, :], in_=pt[:, a, :, :].rearrange("p u r -> p (u r)"),
                            func=ACT.Identity, scale=gb[:, sl : sl + 1], bias=gb[:, 32 + sl : 33 + sl],
                        )

            def interleave(r, first, last):
                n = last - first
                zi = zpool.tile([P, 2, 256, 4], BF16, name="zi", align_bytes=64)
                zis[(r, first)] = zi
                nc.vector.tensor_copy(
                    out=zi[:, 0:n].rearrange("p g (c i) t -> p (g c) t i", i=4),
                    in_=zps[(r, first)][:, :, 0:n].rearrange("p t g (c i) -> p (g c) t i", i=4),
                )

            def quantise(r, first, last):
                n = last - first
                zc, zs = codes[r]
                nc.vector.quantize_mx(
                    out=zc[:, first:last, :].rearrange("p g c -> p (g c)").bitcast(FP8X4),
                    scales=zs[:, first:last, :].rearrange("p g c -> p (g c)"),
                    in_=zis[(r, first)][:, 0:n].rearrange("p g c t -> p (g c t)"),
                )

            def multiply(r):
                zc, zs = codes[r]
                for u in range(2):
                    acc = psm.tile([P, DIM], F32, name="acc")
                    accs[(r, u)] = acc
                    for g5 in range(5):
                        nc.tensor.matmul_mx(
                            out=acc[:],
                            lhsT=zc[:, g5, P * u : P * u + P].bitcast(FP8X4),
                            lhsT_scale=zs[:, g5, P * u : P * u + P],
                            rhs=wc[:, g5, :].bitcast(FP8X4),
                            rhs_scale=ws[:, g5, :],
                            start=(g5 == 0),
                            stop=(g5 == 4),
                        )

            def add_up(r, u):
                tb = tbs[r]
                nc.vector.tensor_tensor(out=tb[:, u, :], in0=accs[(r, u)][:], in1=tb[:, u, :], op=ALU.add)
                if r == 15:
                    nc.sync.dma_start(out=out_v[:, u, r, :], in_=tb[:, u, :])
                elif u == 1:
                    nc.sync.dma_start(out=out_v[:, :, r, :], in_=tb[:])

            for s in range(5):
                norm(0, 0, s)
                norm(0, 1, s)
            late = cell_sums(ORDER[6] // 2, EARLY + 1, 16) + last_sums(EARLY, 16)
            late = [late[0:3], late[3:6], late[6:8], late[8:10], late[10:11], late[11:13]]
            for r in range(16):
                if 2 <= r < 15:
                    load(r + 1)
                zc_t = cpool.tile([P, 5, 256], U32, name="zc", align_bytes=64)
                zs_t = cpool.tile([P, 5, 256], U8, name="zs", align_bytes=64)
                codes[r] = (zc_t, zs_t)
                for n, (first, last) in enumerate(GROUPS):
                    zp = zpool.tile([P, 4, 2, 256], BF16, name="zp")
                    zps[(r, first)] = zp
                    for g5 in range(first, last):
                        turn(r, g5, zp[:, :, g5 - first])
                    if n == 1 and r >= 1:
                        multiply(r - 1)
                    if n == 2 and r >= 1:
                        add_up(r - 1, 0)
                    if r < 15:
                        for e, part in BEFORE[n]:
                            norm(r + 1, e, part)
                    interleave(r, first, last)
                    if r < 15:
                        for e, part in AFTER[n]:
                            norm(r + 1, e, part)
                    if n == 2 and r >= 1:
                        add_up(r - 1, 1)
                    if r == 0:
                        quantise_w(2 + n)
                    quantise(r, first, last)
                    if r < 2:
                        for step in late[3 * r + n]:
                            step()
                if 2 <= r < 15:
                    add_bias(r + 1)
            multiply(15)
            add_up(15, 0)
            add_up(15, 1)
